import numpy as np
import ml_dtypes


def mxq(x, axis, fmt="e4m3"):
    dtype, down = {"e4m3": (ml_dtypes.float8_e4m3fn, 7), "e5m2": (ml_dtypes.float8_e5m2, 14)}[fmt]
    v = np.moveaxis(np.asarray(x, np.float32).astype(ml_dtypes.bfloat16).astype(np.float64), axis, -1)
    blocks = v.reshape(v.shape[:-1] + (-1, 32))
    amax = np.abs(blocks).max(-1, keepdims=True)
    byte = np.maximum(np.where(amax > 0, np.frexp(amax)[1] - 1 + 127, 0) - down, 1)
    scale = np.exp2(byte - 127.0)
    codes = (blocks / scale).astype(np.float32).astype(dtype).astype(np.float64)
    return np.moveaxis((codes * scale).reshape(v.shape), -1, axis)


WIDE = False


def mx_kscale(k):
    if not WIDE:
        return np.ones(k)
    levels = np.array([10, -10, 5, -5, 0])
    if k % 512:
        return np.exp2(np.random.permutation(np.resize(levels, k // 32))).repeat(32)
    a = np.empty((k // 512, 16))
    for p in range(k // 512):
        a[p, :8] = np.random.permutation(np.resize(levels, 8))
        for g in range(8):
            far = levels[np.abs(levels - a[p, g]) >= 10]
            a[p, g + 8] = far[np.random.randint(len(far))]
    return np.exp2(a.ravel()).repeat(32)


BF16 = ml_dtypes.bfloat16


def bf(x):
    return np.asarray(x, np.float32).astype(BF16)


def f64(x):
    return np.asarray(x).astype(np.float64)


B, N, E, L, A, H1, H2, G = 256, 8, 8, 384, 128, 1024, 1024, 8


def mish(v):
    return v * np.tanh(np.log(1.0 + np.exp(v)))


def simnorm(v):
    vg = v.reshape(v.shape[:-1] + (v.shape[-1] // G, G))
    ex = np.exp(vg - vg.max(-1, keepdims=True))
    return (ex / ex.sum(-1, keepdims=True)).reshape(v.shape)


def setup_inputs():
    s = mx_kscale(H2)
    r = np.random.standard_normal
    return {"h2": bf(mish(r((B, E, H2))) * s),
            "logits": bf(r((B, N, E))),
            "W3": bf(r((E, H2, L)) * 2.0 / np.sqrt(H2) / s[:, None]),
            "b3": bf(0.3 * r((E, L)))}


def reference(h2, logits, W3, b3):
    hq = mxq(f64(h2).transpose(1, 0, 2), 2, "e4m3")
    z = (hq @ mxq(f64(W3), 1, "e4m3")) + f64(b3)[:, None, :]
    y = simnorm(z)
    lg = f64(logits)
    ex = np.exp(lg - lg.max(-1, keepdims=True))
    comb = ex / ex.sum(-1, keepdims=True)
    return sum(comb[:, :, e, None] * y[e][:, None, :] for e in range(E))

@@ -1,0 +1,411 @@
+from contextlib import ExitStack
+
+import concourse.mybir as mybir
+from concourse.masks import make_identity
+
+F32 = mybir.dt.float32
+BF16 = mybir.dt.bfloat16
+U32 = mybir.dt.uint32
+U8 = mybir.dt.uint8
+FP8X4 = mybir.dt.float8_e4m3fn_x4
+ALU = mybir.AluOpType
+ACT = mybir.ActivationFunctionType
+AX = mybir.AxisListType
+
+P = 128
+B, N, E, L, H2, G8 = 256, 8, 8, 384, 1024, 8
+BT = B // P
+NT = B // 16
+LS = 304
+NLT = 3
+VO = LS - 2 * P
+LV = L - LS
+GP = LS // G8
+GV = LV // G8
+V_UNITS = ((0, 0), (1, 0), (2, 0), (2, 1), (4, 0), (6, 0))
+
+FLOPS = 2 * B * E * H2 * L + 2 * B * N * E * L
+
+
+def bc(ap, a, g):
+    return ap.unsqueeze(3).to_broadcast([P, a, g, G8])
+
+
+def tile_softmoedynamics_pb_kernel(tc, h2, logits, W3, b3, out):
+    nc = tc.nc
+    with ExitStack() as ctx:
+        ctx.enter_context(tc.manual_schedule())
+        const = ctx.enter_context(tc.tile_pool(name="const", bufs=1))
+        raw = ctx.enter_context(tc.tile_pool(name="raw", bufs=4))
+        stage = ctx.enter_context(tc.tile_pool(name="stage", bufs=3))
+        vwork = ctx.enter_context(tc.tile_pool(name="vwork", bufs=3))
+        pwork = ctx.enter_context(tc.tile_pool(name="pwork", bufs=5))
+        psA = ctx.enter_context(tc.psum_pool(name="psA", bufs=3))
+        psB = ctx.enter_context(tc.psum_pool(name="psB", bufs=3))
+        psC = ctx.enter_context(tc.psum_pool(name="psC", bufs=2))
+
+        out2d = out.rearrange("b n l -> (b n) l")
+        h_raw, w_raw, xts, hgs, wgs, codes, zps, tvs, vt, pt = {}, {}, {}, {}, {}, {}, {}, {}, {}, {}
+
+        def load(e):
+            hr = raw.tile([P, BT * H2], BF16, tag="hr")
+            nc.sync.dma_start(
+                out=hr[:].rearrange("p (t k) -> p t k", t=BT),
+                in_=h2[:, e, :].rearrange("(t p) k -> p t k", p=P),
+            )
+            wr = raw.tile([P, 8 * L], BF16, tag="wr")
+            nc.sync.dma_start(
+                out=wr[:].rearrange("p (g r) -> p g r", g=2),
+                in_=W3[e].rearrange("(g p c) w -> p g (c w)", g=2, p=P, c=4),
+            )
+            h_raw[e] = hr
+            w_raw[e] = wr
+
+        ident = const.tile([P, P], F32)
+        mask = const.tile([P, 16], F32)
+        bz = const.tile([P, P], BF16)
+        bz32 = const.tile([P, P], F32)
+        b3T = const.tile([P, 3 * E], F32)
+        lg_b = const.tile([P, BT, N, E], BF16)
+        lg_m = const.tile([P, 1, NT, E], BF16)
+        zT = const.tile([P, NLT, NT, E, 16], F32)
+        zTv = const.tile([P, E, B], F32)
+        comb_b = const.tile([P, BT, N, E], F32)
+        comb_m = const.tile([P, 1, NT, E], F32)
+        ct = const.tile([P, NT * E, 16], F32)
+        c_sb = const.tile([P, NT, P], F32)
+        acc = const.tile([P, BT, N, LV], F32)
+
+        def th(e):
+            hw = h_raw[e][:].bitcast(F32)
+            xts[e] = []
+            for g in range(2):
+                xt = psA.tile([P, 2, B], F32, tag="A")
+                for u in range(2):
+                    for t in range(BT):
+                        c0 = t * 512 + g * 256
+                        nc.tensor.transpose(xt[:, u, t * P : (t + 1) * P], hw[:, c0 + u : c0 + 256 : 2], ident[:])
+                xts[e].append(xt)
+
+        def ch(e):
+            hg = stage.tile([P, 4 * 2 * B], BF16, tag="hg", align_bytes=64)
+            hgf = hg[:].bitcast(F32).rearrange("p (g b u) -> p g b u", g=2, u=2)
+            for g in range(2):
+                nc.scalar.copy(out=hgf[:, g], in_=xts[e][g][:].rearrange("p u b -> p b u"))
+            hgs[e] = hg
+
+        def rg(e, on_vector):
+            if e not in wgs:
+                wg = stage.tile([P, 8 * L], BF16, tag="wg", align_bytes=64)
+                wgs[e] = wg
+            wgv = wgs[e][:].rearrange("p (g w t) -> p g w t", g=2, t=4)
+            wrv = w_raw[e][:].rearrange("p (g t w) -> p g t w", g=2, t=4)
+            for g in range(2):
+                dst = wgv[:, g].rearrange("p (c i) t -> p c t i", i=4)
+                src = wrv[:, g].rearrange("p t (c i) -> p c t i", i=4)
+                if ((e, g) in V_UNITS) == on_vector:
+                    if on_vector:
+                        nc.vector.tensor_copy(out=dst, in_=src)
+                    else:
+                        nc.scalar.copy(out=dst, in_=src)
+
+        def qh(e):
+            hg = hgs[e]
+            hc = stage.tile([P, 2 * B], U32, tag="hc", align_bytes=64)
+            hs = stage.tile([P, 2 * B], U8, tag="hs", align_bytes=64)
+            nc.vector.quantize_mx(out=hc[:].bitcast(FP8X4), scales=hs[:], in_=hg[:])
+            codes[e] = [hc, hs]
+
+        def qw1(e):
+            wg = wgs[e]
+            wc = stage.tile([P, 2 * L], U32, tag="wc", align_bytes=64)
+            ws = stage.tile([P, 2 * L], U8, tag="ws", align_bytes=64)
+            nc.vector.quantize_mx(out=wc[:, 0:512].bitcast(FP8X4), scales=ws[:, 0:512], in_=wg[:, 0:2048])
+            codes[e].extend([wc, ws])
+
+        def qw2(e):
+            wg, wc, ws = wgs[e], codes[e][2], codes[e][3]
+            nc.vector.quantize_mx(
+                out=wc[:, 512:768].bitcast(FP8X4), scales=ws[:, 512:768], in_=wg[:, 2048:3072]
+            )
+
+        def mx(e):
+            hc, hs, wc, ws = codes[e]
+            zps[e] = []
+            for t in range(3):
+                zp = psB.tile([P, B], F32, tag="B")
+                for g in range(2):
+                    c0 = g * L + t * P
+                    nc.tensor.matmul_mx(
+                        out=zp[:],
+                        lhsT=wc[:, c0 : c0 + P].bitcast(FP8X4),
+                        lhsT_scale=ws[:, c0 : c0 + P],
+                        rhs=hc[:, g * B : (g + 1) * B].bitcast(FP8X4),
+                        rhs_scale=hs[:, g * B : (g + 1) * B],
+                        start=(g == 0),
+                        stop=(g == 1),
+                    )
+                zps[e].append(zp)
+
+        def e1(e):
+            for t in range(3):
+                zp = zps[e][t]
+                bias = b3T[:, 3 * e + t : 3 * e + t + 1]
+                nc.scalar.activation(
+                    out=zT[:, t, :, e, :],
+                    in_=zp[:].rearrange("p (t j) -> p t j", j=16),
+                    func=ACT.Identity,
+                    bias=bias,
+                    scale=1.0,
+                )
+                if t == 2:
+                    nc.scalar.activation(out=zTv[:, e, :], in_=zp[:], func=ACT.Identity, bias=bias, scale=1.0)
+
+        def sm_new(pool, pre, src, a, g):
+            return {"pool": pool, "pre": pre, "src": src, "a": a, "g": g}
+
+        def f_max(o):
+            gmax = o["pool"].tile([P, o["a"], o["g"]], F32, tag=o["pre"] + "m")
+            nc.vector.tensor_reduce(out=gmax[:], in_=o["src"], axis=AX.X, op=ALU.max)
+            o["m"] = gmax
+
+        def f_sub(o):
+            ex = o["pool"].tile([P, o["a"], o["g"], G8], F32, tag=o["pre"] + "e")
+            nc.vector.tensor_tensor(out=ex[:], in0=o["src"], in1=bc(o["m"][:], o["a"], o["g"]), op=ALU.subtract)
+            o["e"] = ex
+
+        def f_exp(o):
+            nc.scalar.activation(out=o["e"][:], in_=o["e"][:], func=ACT.Exp)
+
+        def f_sum(o):
+            gsum = o["pool"].tile([P, o["a"], o["g"]], F32, tag=o["pre"] + "s")
+            nc.vector.tensor_reduce(out=gsum[:], in_=o["e"][:], axis=AX.X, op=ALU.add)
+            o["s"] = gsum
+
+        def f_rec(o):
+            rec = o["pool"].tile([P, o["a"], o["g"]], F32, tag=o["pre"] + "r")
+            nc.vector.reciprocal(out=rec[:], in_=o["s"][:])
+            o["r"] = rec
+
+        def f_mul(o, eng, dst):
+            eng.tensor_tensor(out=dst, in0=o["e"][:], in1=bc(o["r"][:], o["a"], o["g"]), op=ALU.mult)
+
+        def tv_(e):
+            tv = psC.tile([P, BT, P], F32, tag="C")
+            for t in range(BT):
+                nc.tensor.transpose(tv[:, t, :], zTv[:, e, t * P : (t + 1) * P], ident[:])
+            tvs[e] = tv
+
+        def v_new(e):
+            vt[e] = sm_new(vwork, "v", tvs[e][:, :, VO:P].rearrange("p t (g c) -> p t g c", c=G8), BT, GV)
+
+        def v_mul(e):
+            f_mul(vt[e], nc.vector, vt[e]["e"][:])
+
+        def v_stt(e, t, n):
+            y = vt[e]["e"][:, t].rearrange("p g c -> p (g c)")
+            w = comb_b[:, t, n, e : e + 1]
+            if e == 0:
+                nc.vector.tensor_scalar_mul(out=acc[:, t, n, :], in0=y, scalar1=w)
+            else:
+                nc.vector.scalar_tensor_tensor(
+                    out=acc[:, t, n, :], in0=y, scalar=w, in1=acc[:, t, n, :], op0=ALU.mult, op1=ALU.add
+                )
+
+        def v_stt_all(e):
+            for t in range(BT):
+                for n in range(N):
+                    v_stt(e, t, n)
+
+        def pc_(q, pool, tag):
+            ctv = ct[:].rearrange("p (t e) j -> p t (e j)", e=E)
+            pc = pool.tile([P, 4, P], F32, tag=tag)
+            for i in range(4):
+                nc.tensor.transpose(pc[:, i, :], ctv[:, 4 * q + i, :], ident[:])
+            return pc
+
+        def cc(q, pc):
+            nc.scalar.copy(out=c_sb[:, 4 * q : 4 * q + 4, :], in_=pc[:])
+
+        def t2(t):
+            zq = psA.tile([P, NLT * P], F32, tag="A")
+            for k in range(NLT):
+                nc.tensor.transpose(
+                    zq[:, k * P : (k + 1) * P], zT[:, k, t].rearrange("p e j -> p (e j)"), ident[:]
+                )
+            pt[t] = [zq]
+
+        def p_new(t):
+            pt[t].append(sm_new(pwork, "p", pt[t][0][:, 0:LS].rearrange("p (o g c) -> p o g c", o=1, c=G8), 1, GP))
+
+        def ml(t):
+            y = pwork.tile([P, 1, GP, G8], F32, tag="y")
+            f_mul(pt[t][1], nc.vector if t == NT - 1 else nc.gpsimd, y[:])
+            pt[t].append(y)
+
+        def mm(t):
+            op = psB.tile([P, LS], F32, tag="B")
+            nc.tensor.matmul(
+                out=op[:], lhsT=c_sb[:, t, :], rhs=pt[t][2][:].rearrange("p o g c -> p (o g c)"), start=True, stop=True
+            )
+            pt[t].append(op)
+
+        def cp(t):
+            osb = pwork.tile([P, LS], F32, tag="o")
+            nc.scalar.copy(out=osb[:], in_=pt[t][3][:])
+            nc.sync.dma_start(out=out2d[t * P : (t + 1) * P, 0:LS], in_=osb[:])
+
+        load(0)
+        nc.vector.memset(bz[:], 0.0)
+        nc.sync.dma_start(out=bz[0 : 3 * E, :], in_=b3.rearrange("e (t l) -> (e t) l", l=P))
+        nc.sync.dma_start(out=lg_b[:], in_=logits.rearrange("(t p) n e -> p t n e", p=P))
+        load(1)
+        nc.sync.dma_start(out=lg_m[:, 0], in_=logits.rearrange("(t j) n e -> (j n) t e", j=16))
+        load(2)
+        load(3)
+        make_identity(nc, ident[:])
+        nc.vector.tensor_reduce(
+            out=mask[:], in_=ident[:].rearrange("p (j n) -> p j n", n=N), axis=AX.X, op=ALU.add
+        )
+        warm = const.tile([P, 1], F32)
+        nc.vector.memset(warm[:], 0.0)
+        nc.scalar.activation(out=warm[:], in_=warm[:], func=ACT.Exp)
+        nc.vector.tensor_copy(out=bz32[:], in_=bz[:])
+        th(0)
+        ch(0)
+        th(1)
+        rg(0, False)
+        sa = sm_new(vwork, "a", lg_b[:], BT, N)
+        sb = sm_new(vwork, "b", lg_m[:], 1, NT)
+
+        def chain(i, lag):
+            k = i - lag
+            if k == 0:
+                return sa
+            if k == 1:
+                return sb
+            if 2 <= k < E + 2:
+                return vt[k - 2]
+            return None
+
+        for i in range(E + 1):
+            if i + 1 < E:
+                ch(i + 1)
+            if chain(i, 1) is not None:
+                f_exp(chain(i, 1))
+            if i + 1 < E:
+                rg(i + 1, False)
+            if 0 <= i - 1:
+                mx(i - 1)
+            if 0 <= i - 2:
+                tv_(i - 2)
+                v_new(i - 2)
+            if i == 0:
+                pb = psC.tile([P, P], F32, tag="C")
+                nc.tensor.transpose(pb[:], bz32[:], ident[:])
+            if i + 2 < E:
+                th(i + 2)
+            if i == E:
+                pc0 = pc_(0, psA, "A")
+            if 0 <= i - 4:
+                v_stt_all(i - 4)
+            if i == 3:
+                for q in range(4):
+                    nc.vector.tensor_tensor(
+                        out=ct[:, 32 * q : 32 * q + 32, :],
+                        in0=comb_m[:, 0, 4 * q : 4 * q + 4, :]
+                        .rearrange("p t e -> p (t e)")
+                        .unsqueeze(2)
+                        .to_broadcast([P, 32, 16]),
+                        in1=mask[:].unsqueeze(1).to_broadcast([P, 32, 16]),
+                        op=ALU.mult,
+                    )
+            if i < E:
+                rg(i, True)
+                qh(i)
+                qw1(i)
+            f_max(chain(i, 0))
+            if chain(i, 1) is not None:
+                f_sum(chain(i, 1))
+            f_sub(chain(i, 0))
+            if chain(i, 1) is not None:
+                f_rec(chain(i, 1))
+            if i < E:
+                qw2(i)
+            if i == 1:
+                f_mul(sa, nc.vector, comb_b[:])
+            if i == 2:
+                f_mul(sb, nc.vector, comb_m[:])
+            if 0 <= i - 3:
+                v_mul(i - 3)
+            if i == 0:
+                nc.vector.tensor_copy(out=b3T[:], in_=pb[:, 0 : 3 * E])
+            if 0 <= i - 1:
+                e1(i - 1)
+            if i == E:
+                cc(0, pc0)
+            if i + 4 < E:
+                load(i + 4)
+
+        f_exp(vt[E - 2])
+        t2(0)
+        t2(1)
+        tv_(E - 1)
+        v_new(E - 1)
+        t2(2)
+
+        def v_block(e, first, count):
+            for k in range(first, first + count):
+                v_stt(e, k // N, k % N)
+                if e == E - 1 and k % N == N - 1:
+                    nc.sync.dma_start(out=out[(k // N) * P : (k // N + 1) * P, :, LS:L], in_=acc[:, k // N])
+
+        pcs = {}
+        for s in range(-1, NT + 3):
+            if 0 <= s and s + 3 < NT:
+                t2(s + 3)
+            if s + 1 < NT:
+                p_new(s + 1)
+                f_max(pt[s + 1][1])
+            if s == -1:
+                f_max(vt[E - 1])
+            if s == 0:
+                f_sub(vt[E - 1])
+                f_exp(vt[E - 1])
+            if s == 2:
+                f_sum(vt[E - 1])
+            if 0 <= s - 1 < NT:
+                f_sum(pt[s - 1][1])
+            if s == -1:
+                f_sum(vt[E - 2])
+            if s == 0:
+                f_rec(vt[E - 2])
+            if s == 3:
+                f_rec(vt[E - 1])
+            if s + 1 < NT:
+                f_sub(pt[s + 1][1])
+                f_exp(pt[s + 1][1])
+            if 0 <= s - 1 < NT:
+                f_rec(pt[s - 1][1])
+            if s == NT:
+                v_block(E - 1, 0, 4)
+            if 0 <= s - 1 < NT:
+                ml(s - 1)
+            if s == 1:
+                v_block(E - 3, 0, 16)
+                v_mul(E - 2)
+            if s == 7:
+                v_block(E - 2, 0, 16)
+                v_mul(E - 1)
+            if s == NT:
+                v_block(E - 1, 4, 12)
+            if 0 <= s - 2 < NT:
+                mm(s - 2)
+            if s in (0, 3, 6):
+                q = s // 3 + 1
+                pcs[q] = pc_(q, psC, "C")
+            if 0 <= s - 3 < NT:
+                cp(s - 3)
+            if s in (1, 4, 7):
+                q = s // 3 + 1
+                cc(q, pcs[q])

@@ -16,13 +16,17 @@ P = 128
 B, N, E, L, H2, G8 = 256, 8, 8, 384, 1024, 8
 BT = B // P
 NT = B // 16
-LS = 304
-NLT = 3
-VO = LS - 2 * P
-LV = L - LS
-GP = LS // G8
+VO = 48
+LV = P - VO
+LS = L - LV
 GV = LV // G8
-V_UNITS = ((0, 0), (1, 0), (2, 0), (2, 1), (4, 0), (6, 0))
+LAB = P + VO
+CA, CB, CC = 2, 1, 0
+V_SLOTS = ((CA, 0), (CB, 0), (CB, 1), (CB, 2), (CB,3), (CB, 4), (CB, 5))
+SLOTS = [(c, e) for e in range(E) for c in (CA, CB)] + [(CC, e) for e in range(E)]
+P_EVERY = {CA: 1, CB: 1, CC: 1}
+V_LAG, X_LAG, S_LAG, M_LAG = 3, 1, 2, 2
+F1, F2, F3, KEEP, PC0 = 4, 4, 4, 32, 9
 
 FLOPS = 2 * B * E * H2 * L + 2 * B * N * E * L
 
@@ -34,31 +38,36 @@ def bc(ap, a, g):
 def tile_softmoedynamics_pb_kernel(tc, h2, logits, W3, b3, out):
     nc = tc.nc
     with ExitStack() as ctx:
-        ctx.enter_context(tc.manual_schedule())
+        ENG = mybir.EngineType
+        ctx.enter_context(tc.manual_schedule(engines={ENG.PE, ENG.Activation, ENG.SP, ENG.Pool}))
         const = ctx.enter_context(tc.tile_pool(name="const", bufs=1))
-        raw = ctx.enter_context(tc.tile_pool(name="raw", bufs=4))
+        rawh = ctx.enter_context(tc.tile_pool(name="rawh", bufs=4))
+        raww = ctx.enter_context(tc.tile_pool(name="raww", bufs=8))
         stage = ctx.enter_context(tc.tile_pool(name="stage", bufs=3))
+        hcode = ctx.enter_context(tc.tile_pool(name="hcode", bufs=8))
         vwork = ctx.enter_context(tc.tile_pool(name="vwork", bufs=3))
-        pwork = ctx.enter_context(tc.tile_pool(name="pwork", bufs=5))
+        pwork = ctx.enter_context(tc.tile_pool(name="pwork", bufs=4))
         psA = ctx.enter_context(tc.psum_pool(name="psA", bufs=3))
-        psB = ctx.enter_context(tc.psum_pool(name="psB", bufs=3))
-        psC = ctx.enter_context(tc.psum_pool(name="psC", bufs=2))
+        psB = ctx.enter_context(tc.psum_pool(name="psB", bufs=2))
+        psC = ctx.enter_context(tc.psum_pool(name="psC", bufs=3))
 
         out2d = out.rearrange("b n l -> (b n) l")
-        h_raw, w_raw, xts, hgs, wgs, codes, zps, tvs, vt, pt = {}, {}, {}, {}, {}, {}, {}, {}, {}, {}
+        h_raw, w_raw, xts, hgs, wgs, hcodes, wcodes, zps, tvs, vt, pt = {}, {}, {}, {}, {}, {}, {}, {}, {}, {}, {}
 
-        def load(e):
-            hr = raw.tile([P, BT * H2], BF16, tag="hr")
+        def load_h(e):
+            hr = rawh.tile([P, BT * H2], BF16, tag="hr")
             nc.sync.dma_start(
                 out=hr[:].rearrange("p (t k) -> p t k", t=BT),
                 in_=h2[:, e, :].rearrange("(t p) k -> p t k", p=P),
             )
-            wr = raw.tile([P, 8 * L], BF16, tag="wr")
+            h_raw[e] = hr
+
+        def load_w(e):
+            wr = raww.tile([P, 8 * L], BF16, tag="wr")
             nc.sync.dma_start(
                 out=wr[:].rearrange("p (g r) -> p g r", g=2),
                 in_=W3[e].rearrange("(g p c) w -> p g (c w)", g=2, p=P, c=4),
             )
-            h_raw[e] = hr
             w_raw[e] = wr
 
         ident = const.tile([P, P], F32)
@@ -68,13 +77,15 @@ def tile_softmoedynamics_pb_kernel(tc, h2, logits, W3, b3, out):
         b3T = const.tile([P, 3 * E], F32)
         lg_b = const.tile([P, BT, N, E], BF16)
         lg_m = const.tile([P, 1, NT, E], BF16)
-        zT = const.tile([P, NLT, NT, E, 16], F32)
+        zT = const.tile([P, 3, NT, E, 16], F32)
         zTv = const.tile([P, E, B], F32)
         comb_b = const.tile([P, BT, N, E], F32)
         comb_m = const.tile([P, 1, NT, E], F32)
         ct = const.tile([P, NT * E, 16], F32)
         c_sb = const.tile([P, NT, P], F32)
         acc = const.tile([P, BT, N, LV], F32)
+        y_ab = const.tile([P, NT, LAB], F32)
+        y_c = const.tile([P, NT, P], F32)
 
         def th(e):
             hw = h_raw[e][:].bitcast(F32)
@@ -94,72 +105,61 @@ def tile_softmoedynamics_pb_kernel(tc, h2, logits, W3, b3, out):
                 nc.scalar.copy(out=hgf[:, g], in_=xts[e][g][:].rearrange("p u b -> p b u"))
             hgs[e] = hg
 
-        def rg(e, on_vector):
-            if e not in wgs:
-                wg = stage.tile([P, 8 * L], BF16, tag="wg", align_bytes=64)
-                wgs[e] = wg
-            wgv = wgs[e][:].rearrange("p (g w t) -> p g w t", g=2, t=4)
-            wrv = w_raw[e][:].rearrange("p (g t w) -> p g t w", g=2, t=4)
-            for g in range(2):
-                dst = wgv[:, g].rearrange("p (c i) t -> p c t i", i=4)
-                src = wrv[:, g].rearrange("p t (c i) -> p c t i", i=4)
-                if ((e, g) in V_UNITS) == on_vector:
-                    if on_vector:
-                        nc.vector.tensor_copy(out=dst, in_=src)
-                    else:
-                        nc.scalar.copy(out=dst, in_=src)
+        def rg(s, on_vector):
+            if (s in V_SLOTS) != on_vector:
+                return
+            c, e = s
+            wg = stage.tile([P, 8 * P], BF16, tag="wg", align_bytes=64)
+            wgs[s] = wg
+            dst = wg[:].rearrange("p (g c i t) -> p g c t i", g=2, i=4, t=4)
+            src = w_raw[e][:].rearrange("p (g t w) -> p g t w", g=2, t=4)[:, :, :, c * P : (c + 1) * P]
+            src = src.rearrange("p g t (c i) -> p g c t i", i=4)
+            if on_vector:
+                nc.vector.tensor_copy(out=dst, in_=src)
+            else:
+                nc.scalar.copy(out=dst, in_=src)
 
         def qh(e):
-            hg = hgs[e]
-            hc = stage.tile([P, 2 * B], U32, tag="hc", align_bytes=64)
-            hs = stage.tile([P, 2 * B], U8, tag="hs", align_bytes=64)
-            nc.vector.quantize_mx(out=hc[:].bitcast(FP8X4), scales=hs[:], in_=hg[:])
-            codes[e] = [hc, hs]
+            hc = hcode.tile([P, 2 * B], U32, tag="hc", align_bytes=64)
+            hs = hcode.tile([P, 2 * B], U8, tag="hs", align_bytes=64)
+            nc.vector.quantize_mx(out=hc[:].bitcast(FP8X4), scales=hs[:], in_=hgs[e][:])
+            hcodes[e] = (hc, hs)
 
-        def qw1(e):
-            wg = wgs[e]
-            wc = stage.tile([P, 2 * L], U32, tag="wc", align_bytes=64)
-            ws = stage.tile([P, 2 * L], U8, tag="ws", align_bytes=64)
-            nc.vector.quantize_mx(out=wc[:, 0:512].bitcast(FP8X4), scales=ws[:, 0:512], in_=wg[:, 0:2048])
-            codes[e].extend([wc, ws])
+        def qw(s):
+            wc = stage.tile([P, 2 * P], U32, tag="wc", align_bytes=64)
+            ws = stage.tile([P, 2 * P], U8, tag="ws", align_bytes=64)
+            nc.vector.quantize_mx(out=wc[:].bitcast(FP8X4), scales=ws[:], in_=wgs[s][:])
+            wcodes[s] = (wc, ws)
 
-        def qw2(e):
-            wg, wc, ws = wgs[e], codes[e][2], codes[e][3]
-            nc.vector.quantize_mx(
-                out=wc[:, 512:768].bitcast(FP8X4), scales=ws[:, 512:768], in_=wg[:, 2048:3072]
-            )
-
-        def mx(e):
-            hc, hs, wc, ws = codes[e]
-            zps[e] = []
-            for t in range(3):
-                zp = psB.tile([P, B], F32, tag="B")
-                for g in range(2):
-                    c0 = g * L + t * P
-                    nc.tensor.matmul_mx(
-                        out=zp[:],
-                        lhsT=wc[:, c0 : c0 + P].bitcast(FP8X4),
-                        lhsT_scale=ws[:, c0 : c0 + P],
-                        rhs=hc[:, g * B : (g + 1) * B].bitcast(FP8X4),
-                        rhs_scale=hs[:, g * B : (g + 1) * B],
-                        start=(g == 0),
-                        stop=(g == 1),
-                    )
-                zps[e].append(zp)
-
-        def e1(e):
-            for t in range(3):
-                zp = zps[e][t]
-                bias = b3T[:, 3 * e + t : 3 * e + t + 1]
-                nc.scalar.activation(
-                    out=zT[:, t, :, e, :],
-                    in_=zp[:].rearrange("p (t j) -> p t j", j=16),
-                    func=ACT.Identity,
-                    bias=bias,
-                    scale=1.0,
+        def mx(s):
+            hc, hs = hcodes[s[1]]
+            wc, ws = wcodes[s]
+            zp = psB.tile([P, B], F32, tag="B")
+            for g in range(2):
+                nc.tensor.matmul_mx(
+                    out=zp[:],
+                    lhsT=wc[:, g * P : (g + 1) * P].bitcast(FP8X4),
+                    lhsT_scale=ws[:, g * P : (g + 1) * P],
+                    rhs=hc[:, g * B : (g + 1) * B].bitcast(FP8X4),
+                    rhs_scale=hs[:, g * B : (g + 1) * B],
+                    start=(g == 0),
+                    stop=(g == 1),
                 )
-                if t == 2:
-                    nc.scalar.activation(out=zTv[:, e, :], in_=zp[:], func=ACT.Identity, bias=bias, scale=1.0)
+            zps[s] = zp
+
+        def e1(s):
+            c, e = s
+            zp = zps[s]
+            bias = b3T[:, 3 * e + c : 3 * e + c + 1]
+            if c == CA:
+                nc.scalar.activation(out=zTv[:, e, :], in_=zp[:], func=ACT.Identity, bias=bias, scale=1.0)
+            nc.scalar.activation(
+                out=zT[:, c, :, e, :],
+                in_=zp[:].rearrange("p (t j) -> p t j", j=16),
+                func=ACT.Identity,
+                bias=bias,
+                scale=1.0,
+            )
 
         def sm_new(pool, pre, src, a, g):
             return {"pool": pool, "pre": pre, "src": src, "a": a, "g": g}
@@ -190,20 +190,15 @@ def tile_softmoedynamics_pb_kernel(tc, h2, logits, W3, b3, out):
         def f_mul(o, eng, dst):
             eng.tensor_tensor(out=dst, in0=o["e"][:], in1=bc(o["r"][:], o["a"], o["g"]), op=ALU.mult)
 
-        def tv_(e):
-            tv = psC.tile([P, BT, P], F32, tag="C")
-            for t in range(BT):
-                nc.tensor.transpose(tv[:, t, :], zTv[:, e, t * P : (t + 1) * P], ident[:])
-            tvs[e] = tv
-
-        def v_new(e):
-            vt[e] = sm_new(vwork, "v", tvs[e][:, :, VO:P].rearrange("p t (g c) -> p t g c", c=G8), BT, GV)
-
-        def v_mul(e):
-            f_mul(vt[e], nc.vector, vt[e]["e"][:])
+        def tv_(k):
+            tv = psC.tile([P, 2, BT, P], F32, tag="C")
+            for d in range(2):
+                for t in range(BT):
+                    nc.tensor.transpose(tv[:, d, t, :], zTv[:, 2 * k + d, t * P : (t + 1) * P], ident[:])
+            vt[k] = sm_new(vwork, "v", tv[:, :, :, VO:P].rearrange("p d t (g c) -> p (d t) g c", c=G8), 2 * BT, GV)
 
         def v_stt(e, t, n):
-            y = vt[e]["e"][:, t].rearrange("p g c -> p (g c)")
+            y = vt[e // 2]["e"][:, (e % 2) * BT + t].rearrange("p g c -> p (g c)")
             w = comb_b[:, t, n, e : e + 1]
             if e == 0:
                 nc.vector.tensor_scalar_mul(out=acc[:, t, n, :], in0=y, scalar1=w)
@@ -216,10 +211,12 @@ def tile_softmoedynamics_pb_kernel(tc, h2, logits, W3, b3, out):
             for t in range(BT):
                 for n in range(N):
                     v_stt(e, t, n)
+                if e == E - 1:
+                    nc.sync.dma_start(out=out[t * P : (t + 1) * P, :, LS:L], in_=acc[:, t])
 
-        def pc_(q, pool, tag):
+        def pc_(q):
             ctv = ct[:].rearrange("p (t e) j -> p t (e j)", e=E)
-            pc = pool.tile([P, 4, P], F32, tag=tag)
+            pc = psC.tile([P, 4, P], F32, tag="C")
             for i in range(4):
                 nc.tensor.transpose(pc[:, i, :], ctv[:, 4 * q + i, :], ident[:])
             return pc
@@ -227,42 +224,55 @@ def tile_softmoedynamics_pb_kernel(tc, h2, logits, W3, b3, out):
         def cc(q, pc):
             nc.scalar.copy(out=c_sb[:, 4 * q : 4 * q + 4, :], in_=pc[:])
 
-        def t2(t):
-            zq = psA.tile([P, NLT * P], F32, tag="A")
-            for k in range(NLT):
-                nc.tensor.transpose(
-                    zq[:, k * P : (k + 1) * P], zT[:, k, t].rearrange("p e j -> p (e j)"), ident[:]
-                )
-            pt[t] = [zq]
-
-        def p_new(t):
-            pt[t].append(sm_new(pwork, "p", pt[t][0][:, 0:LS].rearrange("p (o g c) -> p o g c", o=1, c=G8), 1, GP))
-
-        def ml(t):
-            y = pwork.tile([P, 1, GP, G8], F32, tag="y")
-            f_mul(pt[t][1], nc.vector if t == NT - 1 else nc.gpsimd, y[:])
-            pt[t].append(y)
-
-        def mm(t):
-            op = psB.tile([P, LS], F32, tag="B")
-            nc.tensor.matmul(
-                out=op[:], lhsT=c_sb[:, t, :], rhs=pt[t][2][:].rearrange("p o g c -> p (o g c)"), start=True, stop=True
+        def t2(c, q):
+            zq = psA.tile([P, 4, P], F32, tag="A")
+            for i in range(4):
+                nc.tensor.transpose(zq[:, i, :], zT[:, c, 4 * q + i].rearrange("p e j -> p (e j)"), ident[:])
+            w = VO if c == CA else P
+            pt[c, q] = sm_new(
+                pwork, "p%d" % (c == CA), zq[:, :, 0:w].rearrange("p i (g c) -> p i g c", c=G8), 4, w // G8
             )
-            pt[t].append(op)
 
-        def cp(t):
-            osb = pwork.tile([P, LS], F32, tag="o")
-            nc.scalar.copy(out=osb[:], in_=pt[t][3][:])
-            nc.sync.dma_start(out=out2d[t * P : (t + 1) * P, 0:LS], in_=osb[:])
+        def ml(c, q, eng):
+            t0 = slice(4 * q, 4 * q + 4)
+            dst = y_c[:, t0, :] if c == CC else y_ab[:, t0, 0:P] if c == CB else y_ab[:, t0, P:LAB]
+            f_mul(pt[c, q], eng, dst.rearrange("p i (g c) -> p i g c", c=G8))
 
-        load(0)
+        def mm_ab(k):
+            op = psC.tile([P, 2, LAB], F32, tag="C")
+            for i in range(2):
+                t = 2 * k + i
+                nc.tensor.matmul(out=op[:, i, :], lhsT=c_sb[:, t, :], rhs=y_ab[:, t, :], start=True, stop=True)
+            return op
+
+        def cp_ab(k, op):
+            osb = pwork.tile([P, 2, LAB], F32, tag="oab")
+            nc.scalar.copy(out=osb[:], in_=op[:])
+            rows = out2d[2 * k * P : (2 * k + 2) * P, P : P + LAB]
+            nc.sync.dma_start(out=rows.rearrange("(t p) l -> p t l", p=P), in_=osb[:])
+
+        def mm_c(q):
+            op = psC.tile([P, 4, P], F32, tag="C")
+            for i in range(4):
+                t = 4 * q + i
+                nc.tensor.matmul(out=op[:, i, :], lhsT=c_sb[:, t, :], rhs=y_c[:, t, :], start=True, stop=True)
+            return op
+
+        def cp_c(q, op):
+            osb = pwork.tile([P, 4, P], F32, tag="oc")
+            nc.scalar.copy(out=osb[:], in_=op[:])
+            rows = out2d[4 * q * P : (4 * q + 4) * P, 0:P]
+            nc.sync.dma_start(out=rows.rearrange("(t p) l -> p t l", p=P), in_=osb[:])
+
+        load_h(0)
+        nc.sync.dma_start(out=lg_m[:, 0], in_=logits.rearrange("(t j) n e -> (j n) t e", j=16))
+        nc.sync.dma_start(out=lg_b[:], in_=logits.rearrange("(t p) n e -> p t n e", p=P))
+        load_w(0)
         nc.vector.memset(bz[:], 0.0)
         nc.sync.dma_start(out=bz[0 : 3 * E, :], in_=b3.rearrange("e (t l) -> (e t) l", l=P))
-        nc.sync.dma_start(out=lg_b[:], in_=logits.rearrange("(t p) n e -> p t n e", p=P))
-        load(1)
-        nc.sync.dma_start(out=lg_m[:, 0], in_=logits.rearrange("(t j) n e -> (j n) t e", j=16))
-        load(2)
-        load(3)
+        for e in range(1, 4):
+            load_h(e)
+            load_w(e)
         make_identity(nc, ident[:])
         nc.vector.tensor_reduce(
             out=mask[:], in_=ident[:].rearrange("p (j n) -> p j n", n=N), axis=AX.X, op=ALU.add
@@ -270,46 +280,131 @@ def tile_softmoedynamics_pb_kernel(tc, h2, logits, W3, b3, out):
         warm = const.tile([P, 1], F32)
         nc.vector.memset(warm[:], 0.0)
         nc.scalar.activation(out=warm[:], in_=warm[:], func=ACT.Exp)
-        nc.vector.tensor_copy(out=bz32[:], in_=bz[:])
         th(0)
-        ch(0)
-        th(1)
-        rg(0, False)
+        load_h(4)
+        load_w(4)
         sa = sm_new(vwork, "a", lg_b[:], BT, N)
         sb = sm_new(vwork, "b", lg_m[:], 1, NT)
+        f_max(sb)
+        f_max(sa)
+        f_sub(sb)
+        f_sub(sa)
+        ch(0)
+        f_exp(sb)
+        f_exp(sa)
+        th(1)
+        load_h(5)
+        load_w(5)
+        rg(SLOTS[0], False)
+        nc.vector.tensor_copy(out=bz32[:], in_=bz[:])
 
-        def chain(i, lag):
-            k = i - lag
-            if k == 0:
-                return sa
-            if k == 1:
-                return sb
-            if 2 <= k < E + 2:
-                return vt[k - 2]
-            return None
+        due = {}
 
-        for i in range(E + 1):
-            if i + 1 < E:
-                ch(i + 1)
-            if chain(i, 1) is not None:
-                f_exp(chain(i, 1))
-            if i + 1 < E:
-                rg(i + 1, False)
-            if 0 <= i - 1:
-                mx(i - 1)
-            if 0 <= i - 2:
-                tv_(i - 2)
-                v_new(i - 2)
+        def at(i, what, *args):
+            due.setdefault((i, what), []).append(args)
+
+        for k in range(E // 2):
+            s = SLOTS.index((CA, 2 * k + 1)) + V_LAG
+            at(s - 1, "tv", k)
+            at(s, "new", "v", k)
+            at(s + X_LAG, "exp", "v", k)
+            at(s + S_LAG, "old", "v", k)
+        nexti = 0
+        for c in (CA, CB, CC):
+            nexti = max(SLOTS.index((c, E - 1)) + V_LAG, nexti)
+            for q in range(4):
+                s = nexti
+                at(s - 1, "t2", c, q)
+                at(s, "new", "p", (c, q))
+                at(s + X_LAG, "exp", "p", (c, q))
+                at(s + S_LAG, "old", "p", (c, q))
+                if c == CB:
+                    for k in (2 * q, 2 * q + 1):
+                        at(s + S_LAG + M_LAG, "mm", mm_ab, cp_ab, k)
+                        at(s + S_LAG + M_LAG + 1, "cp", k)
+                if c == CC:
+                    at(s + S_LAG + M_LAG, "mm", mm_c, cp_c, q)
+                    at(s + S_LAG + M_LAG + 1, "cp", NT + q)
+                nexti += P_EVERY[c]
+        for q in range(4):
+            at(PC0 + q, "pc", q)
+            at(PC0 + q, "cc", q)
+        end = max(i for i, w in due) + 1
+        ops, pcs, stts = {}, {}, []
+        chain = {"v": vt, "p": pt}
+
+        def fill(count):
+            for u in range(min(count, len(stts))):
+                e, t, n = stts.pop(0)
+                v_stt(e, t, n)
+                if e == E - 1 and n == N - 1:
+                    nc.sync.dma_start(out=out[t * P : (t + 1) * P, :, LS:L], in_=acc[:, t])
+
+        for i in range(max(end, len(SLOTS) + 1)):
+            nxt = SLOTS[i + 1] if i + 1 < len(SLOTS) else None
+            cur = SLOTS[i] if i < len(SLOTS) else None
+            prv = SLOTS[i - 1] if 0 <= i - 1 < len(SLOTS) else None
+            if prv:
+                mx(prv)
             if i == 0:
                 pb = psC.tile([P, P], F32, tag="C")
                 nc.tensor.transpose(pb[:], bz32[:], ident[:])
-            if i + 2 < E:
-                th(i + 2)
-            if i == E:
-                pc0 = pc_(0, psA, "A")
-            if 0 <= i - 4:
-                v_stt_all(i - 4)
-            if i == 3:
+            if nxt and nxt[0] == CA and nxt[1] > 0:
+                ch(nxt[1])
+            if nxt:
+                rg(nxt, False)
+            if prv:
+                e1(prv)
+            for kind, k in due.get((i, "exp"), []):
+                f_exp(chain[kind][k])
+            for (k,) in due.get((i, "cp"), []):
+                cpf, kk, op = ops.pop(k)
+                cpf(kk, op)
+            if i + 2 < len(SLOTS) and SLOTS[i + 2][0] == CA and SLOTS[i + 2][1] > 1:
+                e = SLOTS[i + 2][1]
+                th(e)
+                if e + 4 < E:
+                    load_h(e + 4)
+                    load_w(e + 4)
+            for (k,) in due.get((i, "tv"), []):
+                tv_(k)
+            for c, q in due.get((i, "t2"), []):
+                t2(c, q)
+            for f, cpf, k in due.get((i, "mm"), []):
+                ops[k + (NT if cpf is cp_c else 0)] = (cpf, k, f(k))
+            for (q,) in due.get((i, "pc"), []):
+                pcs[q] = pc_(q)
+            for (q,) in due.get((i, "cc"), []):
+                cc(q, pcs.pop(q))
+            new = [chain[kind][k] for kind, k in due.get((i, "new"), [])]
+            old = [chain[kind][k] for kind, k in due.get((i, "old"), [])]
+            if cur:
+                if i == 0:
+                    rg(cur, True)
+                if cur[0] == CA:
+                    qh(cur[1])
+                qw(cur)
+            for o in old:
+                f_sum(o)
+            for o in new:
+                f_max(o)
+            fill(max(0, min(F1, len(stts) - KEEP)))
+            if nxt:
+                rg(nxt, True)
+            for o in old:
+                f_rec(o)
+            for o in new:
+                f_sub(o)
+            fill(max(0, min(F2, len(stts) - KEEP)))
+            if i == 0:
+                f_sum(sb)
+                f_sum(sa)
+                f_rec(sb)
+                f_rec(sa)
+                f_mul(sb, nc.vector, comb_m[:])
+                f_mul(sa, nc.vector, comb_b[:])
+                nc.vector.tensor_copy(out=b3T[:], in_=pb[:, 0 : 3 * E])
+            if i == 1:
                 for q in range(4):
                     nc.vector.tensor_tensor(
                         out=ct[:, 32 * q : 32 * q + 32, :],
@@ -320,92 +415,11 @@ def tile_softmoedynamics_pb_kernel(tc, h2, logits, W3, b3, out):
                         in1=mask[:].unsqueeze(1).to_broadcast([P, 32, 16]),
                         op=ALU.mult,
                     )
-            if i < E:
-                rg(i, True)
-                qh(i)
-                qw1(i)
-            f_max(chain(i, 0))
-            if chain(i, 1) is not None:
-                f_sum(chain(i, 1))
-            f_sub(chain(i, 0))
-            if chain(i, 1) is not None:
-                f_rec(chain(i, 1))
-            if i < E:
-                qw2(i)
-            if i == 1:
-                f_mul(sa, nc.vector, comb_b[:])
-            if i == 2:
-                f_mul(sb, nc.vector, comb_m[:])
-            if 0 <= i - 3:
-                v_mul(i - 3)
-            if i == 0:
-                nc.vector.tensor_copy(out=b3T[:], in_=pb[:, 0 : 3 * E])
-            if 0 <= i - 1:
-                e1(i - 1)
-            if i == E:
-                cc(0, pc0)
-            if i + 4 < E:
-                load(i + 4)
-
-        f_exp(vt[E - 2])
-        t2(0)
-        t2(1)
-        tv_(E - 1)
-        v_new(E - 1)
-        t2(2)
-
-        def v_block(e, first, count):
-            for k in range(first, first + count):
-                v_stt(e, k // N, k % N)
-                if e == E - 1 and k % N == N - 1:
-                    nc.sync.dma_start(out=out[(k // N) * P : (k // N + 1) * P, :, LS:L], in_=acc[:, k // N])
-
-        pcs = {}
-        for s in range(-1, NT + 3):
-            if 0 <= s and s + 3 < NT:
-                t2(s + 3)
-            if s + 1 < NT:
-                p_new(s + 1)
-                f_max(pt[s + 1][1])
-            if s == -1:
-                f_max(vt[E - 1])
-            if s == 0:
-                f_sub(vt[E - 1])
-                f_exp(vt[E - 1])
-            if s == 2:
-                f_sum(vt[E - 1])
-            if 0 <= s - 1 < NT:
-                f_sum(pt[s - 1][1])
-            if s == -1:
-                f_sum(vt[E - 2])
-            if s == 0:
-                f_rec(vt[E - 2])
-            if s == 3:
-                f_rec(vt[E - 1])
-            if s + 1 < NT:
-                f_sub(pt[s + 1][1])
-                f_exp(pt[s + 1][1])
-            if 0 <= s - 1 < NT:
-                f_rec(pt[s - 1][1])
-            if s == NT:
-                v_block(E - 1, 0, 4)
-            if 0 <= s - 1 < NT:
-                ml(s - 1)
-            if s == 1:
-                v_block(E - 3, 0, 16)
-                v_mul(E - 2)
-            if s == 7:
-                v_block(E - 2, 0, 16)
-                v_mul(E - 1)
-            if s == NT:
-                v_block(E - 1, 4, 12)
-            if 0 <= s - 2 < NT:
-                mm(s - 2)
-            if s in (0, 3, 6):
-                q = s // 3 + 1
-                pcs[q] = pc_(q, psC, "C")
-            if 0 <= s - 3 < NT:
-                cp(s - 3)
-            if s in (1, 4, 7):
-                q = s // 3 + 1
-                cc(q, pcs[q])
+            for kind, k in due.get((i, "old"), []):
+                if kind == "v":
+                    f_mul(vt[k], nc.vector, vt[k]["e"][:])
+                    stts.extend([(2 * k + d, t, n) for d in range(2) for t in range(BT) for n in range(N)])
+                else:
+                    ml(*k, nc.vector if k == (CC, 3) else nc.gpsimd)
+            fill(max(0, min(F3, len(stts) - KEEP)))
+        fill(1000)

@@ -25,9 +25,11 @@ CA, CB, CC = 2, 1, 0
 V_SLOTS = ((CA, 0), (CB, 0), (CB, 1), (CB, 2), (CB,3), (CB, 4), (CB, 5))
 SLOTS = [(c, e) for e in range(E) for c in (CA, CB)] + [(CC, e) for e in range(E)]
 P_EVERY = {CA: 1, CB: 1, CC: 1}
-V_LAG, X_LAG, S_LAG, M_LAG = 3, 1, 2, 2
+V_LAG, X_LAG, S_LAG, M_LAG = 2, 1, 2, 2
 F1, F2, F3, KEEP, PC0 = 4, 4, 4, 32, 9
 
+V_MUL = ((CC, 2), (CC, 3))
+N_ST = 4
 FLOPS = 2 * B * E * H2 * L + 2 * B * N * E * L
 
 
@@ -39,7 +41,7 @@ def tile_softmoedynamics_pb_kernel(tc, h2, logits, W3, b3, out):
     nc = tc.nc
     with ExitStack() as ctx:
         ENG = mybir.EngineType
-        ctx.enter_context(tc.manual_schedule(engines={ENG.PE, ENG.Activation, ENG.SP, ENG.Pool}))
+        ctx.enter_context(tc.manual_schedule(engines={ENG.PE, ENG.SP, ENG.Pool}))
         const = ctx.enter_context(tc.tile_pool(name="const", bufs=1))
         rawh = ctx.enter_context(tc.tile_pool(name="rawh", bufs=4))
         raww = ctx.enter_context(tc.tile_pool(name="raww", bufs=8))
@@ -111,13 +113,14 @@ def tile_softmoedynamics_pb_kernel(tc, h2, logits, W3, b3, out):
             c, e = s
             wg = stage.tile([P, 8 * P], BF16, tag="wg", align_bytes=64)
             wgs[s] = wg
-            dst = wg[:].rearrange("p (g c i t) -> p g c t i", g=2, i=4, t=4)
-            src = w_raw[e][:].rearrange("p (g t w) -> p g t w", g=2, t=4)[:, :, :, c * P : (c + 1) * P]
-            src = src.rearrange("p g t (c i) -> p g c t i", i=4)
-            if on_vector:
-                nc.vector.tensor_copy(out=dst, in_=src)
-            else:
-                nc.scalar.copy(out=dst, in_=src)
+            for g in range(2):
+                dst = wg[:, 4 * P * g : 4 * P * (g + 1)].rearrange("p (c i t) -> p c t i", i=4, t=4)
+                src = w_raw[e][:].rearrange("p (g t w) -> p g t w", g=2, t=4)[:, g, :, c * P : (c + 1) * P]
+                src = src.rearrange("p t (c i) -> p c t i", i=4)
+                if on_vector:
+                    nc.vector.tensor_copy(out=dst, in_=src)
+                else:
+                    nc.scalar.copy(out=dst, in_=src)
 
         def qh(e):
             hc = hcode.tile([P, 2 * B], U32, tag="hc", align_bytes=64)
@@ -175,7 +178,8 @@ def tile_softmoedynamics_pb_kernel(tc, h2, logits, W3, b3, out):
             o["e"] = ex
 
         def f_exp(o):
-            nc.scalar.activation(out=o["e"][:], in_=o["e"][:], func=ACT.Exp)
+            with tc.high_priority(offset=1000):
+                nc.scalar.activation(out=o["e"][:], in_=o["e"][:], func=ACT.Exp)
 
         def f_sum(o):
             gsum = o["pool"].tile([P, o["a"], o["g"]], F32, tag=o["pre"] + "s")
@@ -337,8 +341,9 @@ def tile_softmoedynamics_pb_kernel(tc, h2, logits, W3, b3, out):
             for u in range(min(count, len(stts))):
                 e, t, n = stts.pop(0)
                 v_stt(e, t, n)
-                if e == E - 1 and n == N - 1:
-                    nc.sync.dma_start(out=out[t * P : (t + 1) * P, :, LS:L], in_=acc[:, t])
+                if e == E - 1 and n % N_ST == N_ST - 1:
+                    ns = slice(n + 1 - N_ST, n + 1)
+                    nc.sync.dma_start(out=out[t * P : (t + 1) * P, ns, LS:L], in_=acc[:, t, ns])
 
         for i in range(max(end, len(SLOTS) + 1)):
             nxt = SLOTS[i + 1] if i + 1 < len(SLOTS) else None
@@ -420,6 +425,6 @@ def tile_softmoedynamics_pb_kernel(tc, h2, logits, W3, b3, out):
                     f_mul(vt[k], nc.vector, vt[k]["e"][:])
                     stts.extend([(2 * k + d, t, n) for d in range(2) for t in range(BT) for n in range(N)])
                 else:
-                    ml(*k, nc.vector if k == (CC, 3) else nc.gpsimd)
+                    ml(*k, nc.vector if k in V_MUL else nc.gpsimd)
             fill(max(0, min(F3, len(stts) - KEEP)))
         fill(1000)

@@ -22,14 +22,15 @@ LS = L - LV
 GV = LV // G8
 LAB = P + VO
 CA, CB, CC = 2, 1, 0
-V_SLOTS = ((CA, 0), (CB, 0), (CB, 1), (CB, 2), (CB,3), (CB, 4), (CB, 5))
+V_SLOTS = ((CA, 0), (CB, 1), (CB, 2), (CB, 3), (CB, 4), (CB, 5), (CB, 6))
 SLOTS = [(c, e) for e in range(E) for c in (CA, CB)] + [(CC, e) for e in range(E)]
 P_EVERY = {CA: 1, CB: 1, CC: 1}
-V_LAG, X_LAG, S_LAG, M_LAG = 2, 1, 2, 2
-F1, F2, F3, KEEP, PC0 = 4, 4, 4, 32, 9
+V_LAG, X_LAG, S_LAG, M_LAG = 3, 1, 2, 2
+F1, F2, F3, KEEP, PC0 = 0, 0, 8, 40, 9
 
 V_MUL = ((CC, 2), (CC, 3))
 N_ST = 4
+S_ORDER = "cxrep"
 FLOPS = 2 * B * E * H2 * L + 2 * B * N * E * L
 
 
@@ -41,7 +42,7 @@ def tile_softmoedynamics_pb_kernel(tc, h2, logits, W3, b3, out):
     nc = tc.nc
     with ExitStack() as ctx:
         ENG = mybir.EngineType
-        ctx.enter_context(tc.manual_schedule(engines={ENG.PE, ENG.SP, ENG.Pool}))
+        ctx.enter_context(tc.manual_schedule(engines={ENG.PE, ENG.Activation, ENG.SP, ENG.Pool}))
         const = ctx.enter_context(tc.tile_pool(name="const", bufs=1))
         rawh = ctx.enter_context(tc.tile_pool(name="rawh", bufs=4))
         raww = ctx.enter_context(tc.tile_pool(name="raww", bufs=8))
@@ -178,8 +179,7 @@ def tile_softmoedynamics_pb_kernel(tc, h2, logits, W3, b3, out):
             o["e"] = ex
 
         def f_exp(o):
-            with tc.high_priority(offset=1000):
-                nc.scalar.activation(out=o["e"][:], in_=o["e"][:], func=ACT.Exp)
+            nc.scalar.activation(out=o["e"][:], in_=o["e"][:], func=ACT.Exp)
 
         def f_sum(o):
             gsum = o["pool"].tile([P, o["a"], o["g"]], F32, tag=o["pre"] + "s")
@@ -354,17 +354,20 @@ def tile_softmoedynamics_pb_kernel(tc, h2, logits, W3, b3, out):
             if i == 0:
                 pb = psC.tile([P, P], F32, tag="C")
                 nc.tensor.transpose(pb[:], bz32[:], ident[:])
-            if nxt and nxt[0] == CA and nxt[1] > 0:
-                ch(nxt[1])
-            if nxt:
-                rg(nxt, False)
-            if prv:
-                e1(prv)
-            for kind, k in due.get((i, "exp"), []):
-                f_exp(chain[kind][k])
-            for (k,) in due.get((i, "cp"), []):
-                cpf, kk, op = ops.pop(k)
-                cpf(kk, op)
+            for w in S_ORDER:
+                if w == "c" and nxt and nxt[0] == CA and nxt[1] > 0:
+                    ch(nxt[1])
+                if w == "r" and nxt:
+                    rg(nxt, False)
+                if w == "e" and prv:
+                    e1(prv)
+                if w == "x":
+                    for kind, k in due.get((i, "exp"), []):
+                        f_exp(chain[kind][k])
+                if w == "p":
+                    for (k,) in due.get((i, "cp"), []):
+                        cpf, kk, op = ops.pop(k)
+                        cpf(kk, op)
             if i + 2 < len(SLOTS) and SLOTS[i + 2][0] == CA and SLOTS[i + 2][1] > 1:
                 e = SLOTS[i + 2][1]
                 th(e)

@@ -26,7 +26,7 @@ V_SLOTS = ((CA, 0), (CB, 1), (CB, 2), (CB, 3), (CB, 4), (CB, 5), (CB, 6))
 SLOTS = [(c, e) for e in range(E) for c in (CA, CB)] + [(CC, e) for e in range(E)]
 P_EVERY = {CA: 1, CB: 1, CC: 1}
 V_LAG, X_LAG, S_LAG, M_LAG = 3, 1, 2, 2
-F1, F2, F3, KEEP, PC0 = 0, 0, 8, 40, 9
+F1, F2, F3, KEEP, PC0 = 0, 0, 8, 48, 9
 
 V_MUL = ((CC, 2), (CC, 3))
 N_ST = 4
@@ -272,11 +272,14 @@ def tile_softmoedynamics_pb_kernel(tc, h2, logits, W3, b3, out):
         nc.sync.dma_start(out=lg_m[:, 0], in_=logits.rearrange("(t j) n e -> (j n) t e", j=16))
         nc.sync.dma_start(out=lg_b[:], in_=logits.rearrange("(t p) n e -> p t n e", p=P))
         load_w(0)
+        load_h(1)
         nc.vector.memset(bz[:], 0.0)
         nc.sync.dma_start(out=bz[0 : 3 * E, :], in_=b3.rearrange("e (t l) -> (e t) l", l=P))
-        for e in range(1, 4):
-            load_h(e)
-            load_w(e)
+        load_w(1)
+        load_h(2)
+        load_w(2)
+        load_h(3)
+        load_w(3)
         make_identity(nc, ident[:])
         nc.vector.tensor_reduce(
             out=mask[:], in_=ident[:].rearrange("p (j n) -> p j n", n=N), axis=AX.X, op=ALU.add
@@ -314,10 +317,10 @@ def tile_softmoedynamics_pb_kernel(tc, h2, logits, W3, b3, out):
             at(s + X_LAG, "exp", "v", k)
             at(s + S_LAG, "old", "v", k)
         nexti = 0
-        for c in (CA, CB, CC):
+        groups = [(c, q) for q in range(4) for c in (CA, CB)] + [(CC, q) for q in range(4)]
+        for c, q in groups:
             nexti = max(SLOTS.index((c, E - 1)) + V_LAG, nexti)
-            for q in range(4):
-                s = nexti
+            for s in (nexti,):
                 at(s - 1, "t2", c, q)
                 at(s, "new", "p", (c, q))
                 at(s + X_LAG, "exp", "p", (c, q))

@@ -26,7 +26,8 @@ V_SLOTS = ((CA, 0), (CB, 1), (CB, 2), (CB, 3), (CB, 4), (CB, 5), (CB, 6))
 SLOTS = [(c, e) for e in range(E) for c in (CA, CB)] + [(CC, e) for e in range(E)]
 P_EVERY = {CA: 1, CB: 1, CC: 1}
 V_LAG, X_LAG, S_LAG, M_LAG = 3, 1, 2, 2
-F1, F2, F3, KEEP, PC0 = 0, 0, 8, 48, 9
+F1, F2, F3, KEEP = 0, 0, 8, 48
+C_FROM = 15
 
 V_MUL = ((CC, 2), (CC, 3))
 N_ST = 4
@@ -74,17 +75,13 @@ def tile_softmoedynamics_pb_kernel(tc, h2, logits, W3, b3, out):
             w_raw[e] = wr
 
         ident = const.tile([P, P], F32)
-        mask = const.tile([P, 16], F32)
         bz = const.tile([P, P], BF16)
         bz32 = const.tile([P, P], F32)
         b3T = const.tile([P, 3 * E], F32)
         lg_b = const.tile([P, BT, N, E], BF16)
-        lg_m = const.tile([P, 1, NT, E], BF16)
         zT = const.tile([P, 3, NT, E, 16], F32)
         zTv = const.tile([P, E, B], F32)
-        comb_b = const.tile([P, BT, N, E], F32)
-        comb_m = const.tile([P, 1, NT, E], F32)
-        ct = const.tile([P, NT * E, 16], F32)
+        comb = const.tile([P, BT, E, N], F32)
         c_sb = const.tile([P, NT, P], F32)
         acc = const.tile([P, BT, N, LV], F32)
         y_ab = const.tile([P, NT, LAB], F32)
@@ -203,7 +200,7 @@ def tile_softmoedynamics_pb_kernel(tc, h2, logits, W3, b3, out):
 
         def v_stt(e, t, n):
             y = vt[e // 2]["e"][:, (e % 2) * BT + t].rearrange("p g c -> p (g c)")
-            w = comb_b[:, t, n, e : e + 1]
+            w = comb[:, t, e, n : n + 1]
             if e == 0:
                 nc.vector.tensor_scalar_mul(out=acc[:, t, n, :], in0=y, scalar1=w)
             else:
@@ -218,15 +215,18 @@ def tile_softmoedynamics_pb_kernel(tc, h2, logits, W3, b3, out):
                 if e == E - 1:
                     nc.sync.dma_start(out=out[t * P : (t + 1) * P, :, LS:L], in_=acc[:, t])
 
-        def pc_(q):
-            ctv = ct[:].rearrange("p (t e) j -> p t (e j)", e=E)
-            pc = psC.tile([P, 4, P], F32, tag="C")
-            for i in range(4):
-                nc.tensor.transpose(pc[:, i, :], ctv[:, 4 * q + i, :], ident[:])
-            return pc
+        def park():
+            nc.sync.dma_start(
+                out=out.rearrange("(t p) n l -> p t n l", p=P)[:, :, 0, 0 : E * N],
+                in_=comb[:].rearrange("p t e n -> p t (e n)"),
+            )
 
-        def cc(q, pc):
-            nc.scalar.copy(out=c_sb[:, 4 * q : 4 * q + 4, :], in_=pc[:])
+        def load_c(j):
+            rows = out.rearrange("(t j) n l -> j t n l", j=16)[j, :, 0, 0 : E * N]
+            nc.sync.dma_start(
+                out=c_sb[j : P : 16, :, j * N : (j + 1) * N],
+                in_=rows.rearrange("t (e n) -> e t n", e=E),
+            )
 
         def t2(c, q):
             zq = psA.tile([P, 4, P], F32, tag="A")
@@ -269,7 +269,6 @@ def tile_softmoedynamics_pb_kernel(tc, h2, logits, W3, b3, out):
             nc.sync.dma_start(out=rows.rearrange("(t p) l -> p t l", p=P), in_=osb[:])
 
         load_h(0)
-        nc.sync.dma_start(out=lg_m[:, 0], in_=logits.rearrange("(t j) n e -> (j n) t e", j=16))
         nc.sync.dma_start(out=lg_b[:], in_=logits.rearrange("(t p) n e -> p t n e", p=P))
         load_w(0)
         load_h(1)
@@ -281,9 +280,7 @@ def tile_softmoedynamics_pb_kernel(tc, h2, logits, W3, b3, out):
         load_h(3)
         load_w(3)
         make_identity(nc, ident[:])
-        nc.vector.tensor_reduce(
-            out=mask[:], in_=ident[:].rearrange("p (j n) -> p j n", n=N), axis=AX.X, op=ALU.add
-        )
+        nc.gpsimd.memset(c_sb[:], 0.0)
         warm = const.tile([P, 1], F32)
         nc.vector.memset(warm[:], 0.0)
         nc.scalar.activation(out=warm[:], in_=warm[:], func=ACT.Exp)
@@ -291,13 +288,9 @@ def tile_softmoedynamics_pb_kernel(tc, h2, logits, W3, b3, out):
         load_h(4)
         load_w(4)
         sa = sm_new(vwork, "a", lg_b[:], BT, N)
-        sb = sm_new(vwork, "b", lg_m[:], 1, NT)
-        f_max(sb)
         f_max(sa)
-        f_sub(sb)
         f_sub(sa)
         ch(0)
-        f_exp(sb)
         f_exp(sa)
         th(1)
         load_h(5)
@@ -333,11 +326,8 @@ def tile_softmoedynamics_pb_kernel(tc, h2, logits, W3, b3, out):
                     at(s + S_LAG + M_LAG, "mm", mm_c, cp_c, q)
                     at(s + S_LAG + M_LAG + 1, "cp", NT + q)
                 nexti += P_EVERY[c]
-        for q in range(4):
-            at(PC0 + q, "pc", q)
-            at(PC0 + q, "cc", q)
         end = max(i for i, w in due) + 1
-        ops, pcs, stts = {}, {}, []
+        ops, stts = {}, []
         chain = {"v": vt, "p": pt}
 
         def fill(count):
@@ -383,10 +373,9 @@ def tile_softmoedynamics_pb_kernel(tc, h2, logits, W3, b3, out):
                 t2(c, q)
             for f, cpf, k in due.get((i, "mm"), []):
                 ops[k + (NT if cpf is cp_c else 0)] = (cpf, k, f(k))
-            for (q,) in due.get((i, "pc"), []):
-                pcs[q] = pc_(q)
-            for (q,) in due.get((i, "cc"), []):
-                cc(q, pcs.pop(q))
+            if i == C_FROM:
+                for j in range(16):
+                    load_c(j)
             new = [chain[kind][k] for kind, k in due.get((i, "new"), [])]
             old = [chain[kind][k] for kind, k in due.get((i, "old"), [])]
             if cur:
@@ -408,24 +397,16 @@ def tile_softmoedynamics_pb_kernel(tc, h2, logits, W3, b3, out):
                 f_sub(o)
             fill(max(0, min(F2, len(stts) - KEEP)))
             if i == 0:
-                f_sum(sb)
                 f_sum(sa)
-                f_rec(sb)
                 f_rec(sa)
-                f_mul(sb, nc.vector, comb_m[:])
-                f_mul(sa, nc.vector, comb_b[:])
+                nc.vector.tensor_tensor(
+                    out=comb[:],
+                    in0=sa["e"][:].rearrange("p t n e -> p t e n"),
+                    in1=sa["r"][:].unsqueeze(2).to_broadcast([P, BT, E, N]),
+                    op=ALU.mult,
+                )
+                park()
                 nc.vector.tensor_copy(out=b3T[:], in_=pb[:, 0 : 3 * E])
-            if i == 1:
-                for q in range(4):
-                    nc.vector.tensor_tensor(
-                        out=ct[:, 32 * q : 32 * q + 32, :],
-                        in0=comb_m[:, 0, 4 * q : 4 * q + 4, :]
-                        .rearrange("p t e -> p (t e)")
-                        .unsqueeze(2)
-                        .to_broadcast([P, 32, 16]),
-                        in1=mask[:].unsqueeze(1).to_broadcast([P, 32, 16]),
-                        op=ALU.mult,
-                    )
             for kind, k in due.get((i, "old"), []):
                 if kind == "v":
                     f_mul(vt[k], nc.vector, vt[k]["e"][:])

@@ -26,11 +26,11 @@ V_SLOTS = ((CA, 0), (CB, 1), (CB, 2), (CB, 3), (CB, 4), (CB, 5), (CB, 6))
 SLOTS = [(c, e) for e in range(E) for c in (CA, CB)] + [(CC, e) for e in range(E)]
 P_EVERY = {CA: 1, CB: 1, CC: 1}
 V_LAG, X_LAG, S_LAG, M_LAG = 3, 1, 2, 2
-F1, F2, F3, KEEP = 0, 0, 8, 48
+F3, KEEP = 8, 48
 C_FROM = 15
 
-V_MUL = ((CC, 2), (CC, 3))
-N_ST = 4
+V_MUL = ((CC, 3),)
+N_ST = 2
 S_ORDER = "cxrep"
 FLOPS = 2 * B * E * H2 * L + 2 * B * N * E * L
 
@@ -208,13 +208,6 @@ def tile_softmoedynamics_pb_kernel(tc, h2, logits, W3, b3, out):
                     out=acc[:, t, n, :], in0=y, scalar=w, in1=acc[:, t, n, :], op0=ALU.mult, op1=ALU.add
                 )
 
-        def v_stt_all(e):
-            for t in range(BT):
-                for n in range(N):
-                    v_stt(e, t, n)
-                if e == E - 1:
-                    nc.sync.dma_start(out=out[t * P : (t + 1) * P, :, LS:L], in_=acc[:, t])
-
         def park():
             nc.sync.dma_start(
                 out=out.rearrange("(t p) n l -> p t n l", p=P)[:, :, 0, 0 : E * N],
@@ -330,13 +323,13 @@ def tile_softmoedynamics_pb_kernel(tc, h2, logits, W3, b3, out):
         ops, stts = {}, []
         chain = {"v": vt, "p": pt}
 
-        def fill(count):
+        def fill(count, queue):
             for u in range(min(count, len(stts))):
                 e, t, n = stts.pop(0)
                 v_stt(e, t, n)
                 if e == E - 1 and n % N_ST == N_ST - 1:
                     ns = slice(n + 1 - N_ST, n + 1)
-                    nc.sync.dma_start(out=out[t * P : (t + 1) * P, ns, LS:L], in_=acc[:, t, ns])
+                    queue.dma_start(out=out[t * P : (t + 1) * P, ns, LS:L], in_=acc[:, t, ns])
 
         for i in range(max(end, len(SLOTS) + 1)):
             nxt = SLOTS[i + 1] if i + 1 < len(SLOTS) else None
@@ -388,14 +381,12 @@ def tile_softmoedynamics_pb_kernel(tc, h2, logits, W3, b3, out):
                 f_sum(o)
             for o in new:
                 f_max(o)
-            fill(max(0, min(F1, len(stts) - KEEP)))
             if nxt:
                 rg(nxt, True)
             for o in old:
                 f_rec(o)
             for o in new:
                 f_sub(o)
-            fill(max(0, min(F2, len(stts) - KEEP)))
             if i == 0:
                 f_sum(sa)
                 f_rec(sa)
@@ -411,7 +402,9 @@ def tile_softmoedynamics_pb_kernel(tc, h2, logits, W3, b3, out):
                 if kind == "v":
                     f_mul(vt[k], nc.vector, vt[k]["e"][:])
                     stts.extend([(2 * k + d, t, n) for d in range(2) for t in range(BT) for n in range(N)])
+                    if k == E // 2 - 1:
+                        stts[:] = sorted(stts, key=lambda s: (s[1], s[2] // N_ST, s[0], s[2]))
                 else:
                     ml(*k, nc.vector if k in V_MUL else nc.gpsimd)
-            fill(max(0, min(F3, len(stts) - KEEP)))
-        fill(1000)
+            fill(max(0, min(F3, len(stts) - KEEP)), nc.sync)
+        fill(1000, nc.scalar)

@@ -11,400 +11,382 @@ FP8X4 = mybir.dt.float8_e4m3fn_x4
 ALU = mybir.AluOpType
 ACT = mybir.ActivationFunctionType
 AX = mybir.AxisListType
+ENG = mybir.EngineType
 
 P = 128
-B, N, E, L, H2, G8 = 256, 8, 8, 384, 1024, 8
-BT = B // P
-NT = B // 16
-VO = 48
-LV = P - VO
-LS = L - LV
-GV = LV // G8
-LAB = P + VO
-CA, CB, CC = 2, 1, 0
-V_SLOTS = ((CA, 0), (CB, 1), (CB, 2), (CB, 3), (CB, 4), (CB, 5), (CB, 6))
-SLOTS = [(c, e) for e in range(E) for c in (CA, CB)] + [(CC, e) for e in range(E)]
-P_EVERY = {CA: 1, CB: 1, CC: 1}
-V_LAG, X_LAG, S_LAG, M_LAG = 3, 1, 2, 2
-F3, KEEP = 8, 48
-C_FROM = 15
+B, N, E, L, H2 = 256, 8, 8, 384, 1024
+GROUP = 8
+HALVES = B // P
+PASSES = 2
+QUAD = 4
+ROWS = P // E
+TILES = B // ROWS
+TILES_GROUP = 4
 
-V_MUL = ((CC, 3),)
-N_ST = 2
-S_ORDER = "cxrep"
-FLOPS = 2 * B * E * H2 * L + 2 * B * N * E * L
+A, BB, C = 2, 1, 0
+A_TENSOR = 48
+LV = P - A_TENSOR
+AB = P + A_TENSOR
+
+SLOTS = [(c, e) for e in range(E) for c in (A, BB)] + [(C, e) for e in range(E)]
+ON_VECTOR = [(A, 0)] + [(BB, e) for e in range(1, E - 1)]
+
+EXP, NORM, MATMUL = 1, 2, 4
+START = 3
+START_AB = 4
+SOFTMAXES = [(c, q) for h in range(2) for c in (A, BB) for q in (2 * h, 2 * h + 1)] + [(C, q) for q in range(TILES // TILES_GROUP)]
+ADDS_A_SLOT = N
+ADDS_KEPT = 5 * N
+AGENTS_A_STORE = 2
 
 
-def bc(ap, a, g):
-    return ap.unsqueeze(3).to_broadcast([P, a, g, G8])
+def wide(ap, a, g):
+    return ap.unsqueeze(3).to_broadcast([P, a, g, GROUP])
 
 
 def tile_softmoedynamics_pb_kernel(tc, h2, logits, W3, b3, out):
     nc = tc.nc
     with ExitStack() as ctx:
-        ENG = mybir.EngineType
         ctx.enter_context(tc.manual_schedule(engines={ENG.PE, ENG.Activation, ENG.SP, ENG.Pool}))
         const = ctx.enter_context(tc.tile_pool(name="const", bufs=1))
-        rawh = ctx.enter_context(tc.tile_pool(name="rawh", bufs=4))
-        raww = ctx.enter_context(tc.tile_pool(name="raww", bufs=8))
+        raw_h = ctx.enter_context(tc.tile_pool(name="raw_h", bufs=4))
+        raw_w = ctx.enter_context(tc.tile_pool(name="raw_w", bufs=E))
         stage = ctx.enter_context(tc.tile_pool(name="stage", bufs=3))
-        hcode = ctx.enter_context(tc.tile_pool(name="hcode", bufs=8))
+        codes = ctx.enter_context(tc.tile_pool(name="codes", bufs=E))
         vwork = ctx.enter_context(tc.tile_pool(name="vwork", bufs=3))
-        pwork = ctx.enter_context(tc.tile_pool(name="pwork", bufs=4))
-        psA = ctx.enter_context(tc.psum_pool(name="psA", bufs=3))
-        psB = ctx.enter_context(tc.psum_pool(name="psB", bufs=2))
-        psC = ctx.enter_context(tc.psum_pool(name="psC", bufs=3))
-
-        out2d = out.rearrange("b n l -> (b n) l")
-        h_raw, w_raw, xts, hgs, wgs, hcodes, wcodes, zps, tvs, vt, pt = {}, {}, {}, {}, {}, {}, {}, {}, {}, {}, {}
-
-        def load_h(e):
-            hr = rawh.tile([P, BT * H2], BF16, tag="hr")
-            nc.sync.dma_start(
-                out=hr[:].rearrange("p (t k) -> p t k", t=BT),
-                in_=h2[:, e, :].rearrange("(t p) k -> p t k", p=P),
-            )
-            h_raw[e] = hr
-
-        def load_w(e):
-            wr = raww.tile([P, 8 * L], BF16, tag="wr")
-            nc.sync.dma_start(
-                out=wr[:].rearrange("p (g r) -> p g r", g=2),
-                in_=W3[e].rearrange("(g p c) w -> p g (c w)", g=2, p=P, c=4),
-            )
-            w_raw[e] = wr
+        twork = ctx.enter_context(tc.tile_pool(name="twork", bufs=4))
+        ps_in = ctx.enter_context(tc.psum_pool(name="ps_in", bufs=3))
+        ps_z = ctx.enter_context(tc.psum_pool(name="ps_z", bufs=2))
+        ps_out = ctx.enter_context(tc.psum_pool(name="ps_out", bufs=3))
 
         ident = const.tile([P, P], F32)
-        bz = const.tile([P, P], BF16)
-        bz32 = const.tile([P, P], F32)
-        b3T = const.tile([P, 3 * E], F32)
-        lg_b = const.tile([P, BT, N, E], BF16)
-        zT = const.tile([P, 3, NT, E, 16], F32)
-        zTv = const.tile([P, E, B], F32)
-        comb = const.tile([P, BT, E, N], F32)
-        c_sb = const.tile([P, NT, P], F32)
-        acc = const.tile([P, BT, N, LV], F32)
-        y_ab = const.tile([P, NT, LAB], F32)
-        y_c = const.tile([P, NT, P], F32)
+        b_rows = const.tile([P, P], BF16)
+        b_rows32 = const.tile([P, P], F32)
+        bias = const.tile([P, 3 * E], F32)
+        lg = const.tile([P, HALVES, N, E], BF16)
+        route = const.tile([P, HALVES, E, N], F32)
+        diag = const.tile([P, TILES, P], F32)
+        z_tiles = const.tile([P, 3, TILES, E, ROWS], F32)
+        z_rows = const.tile([P, E, B], F32)
+        y_ab = const.tile([P, TILES, AB], F32)
+        y_c = const.tile([P, TILES, P], F32)
+        acc = const.tile([P, HALVES, N, LV], F32)
+        h_raw, h_ps, h_grp, h_mx = {}, {}, {}, {}
+        w_raw, w_grp, w_mx, z_ps = {}, {}, {}, {}
+        soft = {}
+        out2d = out.rearrange("b n l -> (b n) l")
 
-        def th(e):
-            hw = h_raw[e][:].bitcast(F32)
-            xts[e] = []
-            for g in range(2):
-                xt = psA.tile([P, 2, B], F32, tag="A")
+        def load_h(e):
+            raw = raw_h.tile([P, HALVES * H2], BF16, tag="h")
+            h_raw[e] = raw
+            nc.sync.dma_start(
+                out=raw[:].rearrange("p (t k) -> p t k", t=HALVES),
+                in_=h2[:, e, :].rearrange("(t p) k -> p t k", p=P),
+            )
+
+        def load_w(e):
+            raw = raw_w.tile([P, PASSES, QUAD, L], BF16, tag="w")
+            w_raw[e] = raw
+            nc.sync.dma_start(
+                out=raw[:].rearrange("p g c w -> p g (c w)"),
+                in_=W3[e].rearrange("(g p c) w -> p g (c w)", g=PASSES, p=P, c=QUAD),
+            )
+
+        def transpose_h(e):
+            words = h_raw[e][:].bitcast(F32)
+            half, one_pass = H2 // 2, H2 // 2 // PASSES
+            h_ps[e] = []
+            for g in range(PASSES):
+                ps = ps_in.tile([P, 2, B], F32, tag="in")
                 for u in range(2):
-                    for t in range(BT):
-                        c0 = t * 512 + g * 256
-                        nc.tensor.transpose(xt[:, u, t * P : (t + 1) * P], hw[:, c0 + u : c0 + 256 : 2], ident[:])
-                xts[e].append(xt)
+                    for t in range(HALVES):
+                        c0 = t * half + g * one_pass
+                        nc.tensor.transpose(
+                            ps[:, u, t * P : (t + 1) * P], words[:, c0 + u : c0 + one_pass : 2], ident[:]
+                        )
+                h_ps[e].append(ps)
 
-        def ch(e):
-            hg = stage.tile([P, 4 * 2 * B], BF16, tag="hg", align_bytes=64)
-            hgf = hg[:].bitcast(F32).rearrange("p (g b u) -> p g b u", g=2, u=2)
-            for g in range(2):
-                nc.scalar.copy(out=hgf[:, g], in_=xts[e][g][:].rearrange("p u b -> p b u"))
-            hgs[e] = hg
+        def copy_h(e):
+            grp = stage.tile([P, QUAD * PASSES * B], BF16, tag="h", align_bytes=64)
+            h_grp[e] = grp
+            dst = grp[:].bitcast(F32).rearrange("p (g b u) -> p g b u", g=PASSES, u=2)
+            for g in range(PASSES):
+                nc.scalar.copy(out=dst[:, g], in_=h_ps[e][g][:].rearrange("p u b -> p b u"))
 
-        def rg(s, on_vector):
-            if (s in V_SLOTS) != on_vector:
+        def quantise_h(e):
+            c = codes.tile([P, PASSES * B], U32, tag="hc", align_bytes=64)
+            s = codes.tile([P, PASSES * B], U8, tag="hs", align_bytes=64)
+            nc.vector.quantize_mx(out=c[:].bitcast(FP8X4), scales=s[:], in_=h_grp[e][:])
+            h_mx[e] = (c, s)
+
+        def regroup_w(unit, vector):
+            if (unit in ON_VECTOR) != vector:
                 return
-            c, e = s
-            wg = stage.tile([P, 8 * P], BF16, tag="wg", align_bytes=64)
-            wgs[s] = wg
-            for g in range(2):
-                dst = wg[:, 4 * P * g : 4 * P * (g + 1)].rearrange("p (c i t) -> p c t i", i=4, t=4)
-                src = w_raw[e][:].rearrange("p (g t w) -> p g t w", g=2, t=4)[:, g, :, c * P : (c + 1) * P]
-                src = src.rearrange("p t (c i) -> p c t i", i=4)
-                if on_vector:
+            c, e = unit
+            grp = stage.tile([P, PASSES, QUAD * P], BF16, tag="w", align_bytes=64)
+            w_grp[unit] = grp
+            for g in range(PASSES):
+                dst = grp[:, g].rearrange("p (c i t) -> p c t i", i=4, t=QUAD)
+                src = w_raw[e][:, g, :, c * P : (c + 1) * P].rearrange("p t (c i) -> p c t i", i=4)
+                if vector:
                     nc.vector.tensor_copy(out=dst, in_=src)
                 else:
                     nc.scalar.copy(out=dst, in_=src)
 
-        def qh(e):
-            hc = hcode.tile([P, 2 * B], U32, tag="hc", align_bytes=64)
-            hs = hcode.tile([P, 2 * B], U8, tag="hs", align_bytes=64)
-            nc.vector.quantize_mx(out=hc[:].bitcast(FP8X4), scales=hs[:], in_=hgs[e][:])
-            hcodes[e] = (hc, hs)
+        def quantise_w(unit):
+            c = stage.tile([P, PASSES * P], U32, tag="wc", align_bytes=64)
+            s = stage.tile([P, PASSES * P], U8, tag="ws", align_bytes=64)
+            nc.vector.quantize_mx(
+                out=c[:].bitcast(FP8X4), scales=s[:], in_=w_grp[unit][:].rearrange("p g n -> p (g n)")
+            )
+            w_mx[unit] = (c, s)
 
-        def qw(s):
-            wc = stage.tile([P, 2 * P], U32, tag="wc", align_bytes=64)
-            ws = stage.tile([P, 2 * P], U8, tag="ws", align_bytes=64)
-            nc.vector.quantize_mx(out=wc[:].bitcast(FP8X4), scales=ws[:], in_=wgs[s][:])
-            wcodes[s] = (wc, ws)
-
-        def mx(s):
-            hc, hs = hcodes[s[1]]
-            wc, ws = wcodes[s]
-            zp = psB.tile([P, B], F32, tag="B")
-            for g in range(2):
+        def multiply(unit):
+            (hc, hs), (wc, ws) = h_mx[unit[1]], w_mx[unit]
+            z = ps_z.tile([P, B], F32, tag="z")
+            z_ps[unit] = z
+            for g in range(PASSES):
+                w_cols, h_cols = slice(g * P, (g + 1) * P), slice(g * B, (g + 1) * B)
                 nc.tensor.matmul_mx(
-                    out=zp[:],
-                    lhsT=wc[:, g * P : (g + 1) * P].bitcast(FP8X4),
-                    lhsT_scale=ws[:, g * P : (g + 1) * P],
-                    rhs=hc[:, g * B : (g + 1) * B].bitcast(FP8X4),
-                    rhs_scale=hs[:, g * B : (g + 1) * B],
+                    out=z[:],
+                    lhsT=wc[:, w_cols].bitcast(FP8X4),
+                    lhsT_scale=ws[:, w_cols],
+                    rhs=hc[:, h_cols].bitcast(FP8X4),
+                    rhs_scale=hs[:, h_cols],
                     start=(g == 0),
-                    stop=(g == 1),
+                    stop=(g == PASSES - 1),
                 )
-            zps[s] = zp
 
-        def e1(s):
-            c, e = s
-            zp = zps[s]
-            bias = b3T[:, 3 * e + c : 3 * e + c + 1]
-            if c == CA:
-                nc.scalar.activation(out=zTv[:, e, :], in_=zp[:], func=ACT.Identity, bias=bias, scale=1.0)
+        def add_bias(unit):
+            c, e = unit
+            z, b = z_ps[unit], bias[:, 3 * e + c : 3 * e + c + 1]
+            if c == A:
+                nc.scalar.activation(out=z_rows[:, e, :], in_=z[:], func=ACT.Identity, bias=b, scale=1.0)
             nc.scalar.activation(
-                out=zT[:, c, :, e, :],
-                in_=zp[:].rearrange("p (t j) -> p t j", j=16),
+                out=z_tiles[:, c, :, e, :],
+                in_=z[:].rearrange("p (t j) -> p t j", j=ROWS),
                 func=ACT.Identity,
-                bias=bias,
+                bias=b,
                 scale=1.0,
             )
 
-        def sm_new(pool, pre, src, a, g):
-            return {"pool": pool, "pre": pre, "src": src, "a": a, "g": g}
+        def softmax(key, pool, tag, src, a, g):
+            soft[key] = {"pool": pool, "tag": tag, "src": src, "shape": [P, a, g]}
 
-        def f_max(o):
-            gmax = o["pool"].tile([P, o["a"], o["g"]], F32, tag=o["pre"] + "m")
-            nc.vector.tensor_reduce(out=gmax[:], in_=o["src"], axis=AX.X, op=ALU.max)
-            o["m"] = gmax
+        def reduce_to(o, name, src, op):
+            res = o["pool"].tile(o["shape"], F32, tag=o["tag"] + name)
+            nc.vector.tensor_reduce(out=res[:], in_=src, axis=AX.X, op=op)
+            o[name] = res
 
-        def f_sub(o):
-            ex = o["pool"].tile([P, o["a"], o["g"], G8], F32, tag=o["pre"] + "e")
-            nc.vector.tensor_tensor(out=ex[:], in0=o["src"], in1=bc(o["m"][:], o["a"], o["g"]), op=ALU.subtract)
-            o["e"] = ex
+        def subtract(o):
+            _, a, g = o["shape"]
+            res = o["pool"].tile([P, a, g, GROUP], F32, tag=o["tag"] + "e")
+            o["e"] = res
+            nc.vector.tensor_tensor(out=res[:], in0=o["src"], in1=wide(o["max"][:], a, g), op=ALU.subtract)
 
-        def f_exp(o):
+        def exponential(o):
             nc.scalar.activation(out=o["e"][:], in_=o["e"][:], func=ACT.Exp)
 
-        def f_sum(o):
-            gsum = o["pool"].tile([P, o["a"], o["g"]], F32, tag=o["pre"] + "s")
-            nc.vector.tensor_reduce(out=gsum[:], in_=o["e"][:], axis=AX.X, op=ALU.add)
-            o["s"] = gsum
+        def reciprocal(o):
+            res = o["pool"].tile(o["shape"], F32, tag=o["tag"] + "r")
+            nc.vector.reciprocal(out=res[:], in_=o["sum"][:])
+            o["r"] = res
 
-        def f_rec(o):
-            rec = o["pool"].tile([P, o["a"], o["g"]], F32, tag=o["pre"] + "r")
-            nc.vector.reciprocal(out=rec[:], in_=o["s"][:])
-            o["r"] = rec
+        def normalise(o, engine, dst):
+            _, a, g = o["shape"]
+            engine.tensor_tensor(out=dst, in0=o["e"][:], in1=wide(o["r"][:], a, g), op=ALU.mult)
 
-        def f_mul(o, eng, dst):
-            eng.tensor_tensor(out=dst, in0=o["e"][:], in1=bc(o["r"][:], o["a"], o["g"]), op=ALU.mult)
-
-        def tv_(k):
-            tv = psC.tile([P, 2, BT, P], F32, tag="C")
+        def to_rows(k):
+            ps = ps_out.tile([P, 2, HALVES, P], F32, tag="out")
             for d in range(2):
-                for t in range(BT):
-                    nc.tensor.transpose(tv[:, d, t, :], zTv[:, 2 * k + d, t * P : (t + 1) * P], ident[:])
-            vt[k] = sm_new(vwork, "v", tv[:, :, :, VO:P].rearrange("p d t (g c) -> p (d t) g c", c=G8), 2 * BT, GV)
+                for t in range(HALVES):
+                    nc.tensor.transpose(ps[:, d, t, :], z_rows[:, 2 * k + d, t * P : (t + 1) * P], ident[:])
+            src = ps[:, :, :, A_TENSOR:P].rearrange("p d t (g c) -> p (d t) g c", c=GROUP)
+            softmax(("rows", k), vwork, "v", src, 2 * HALVES, LV // GROUP)
 
-        def v_stt(e, t, n):
-            y = vt[e // 2]["e"][:, (e % 2) * BT + t].rearrange("p g c -> p (g c)")
-            w = comb[:, t, e, n : n + 1]
+        def multiply_add(e, t, n):
+            y = soft["rows", e // 2]["e"][:, (e % 2) * HALVES + t].rearrange("p g c -> p (g c)")
+            weight, a = route[:, t, e, n : n + 1], acc[:, t, n, :]
             if e == 0:
-                nc.vector.tensor_scalar_mul(out=acc[:, t, n, :], in0=y, scalar1=w)
+                nc.vector.tensor_scalar_mul(out=a, in0=y, scalar1=weight)
             else:
-                nc.vector.scalar_tensor_tensor(
-                    out=acc[:, t, n, :], in0=y, scalar=w, in1=acc[:, t, n, :], op0=ALU.mult, op1=ALU.add
-                )
+                nc.vector.scalar_tensor_tensor(out=a, in0=y, scalar=weight, in1=a, op0=ALU.mult, op1=ALU.add)
 
-        def park():
+        adds = []
+
+        def multiply_adds(count, queue):
+            for _ in range(count):
+                e, t, n = adds.pop(0)
+                multiply_add(e, t, n)
+                if e == E - 1 and n % AGENTS_A_STORE == AGENTS_A_STORE - 1:
+                    ns = slice(n + 1 - AGENTS_A_STORE, n + 1)
+                    queue.dma_start(out=out[t * P : (t + 1) * P, ns, L - LV : L], in_=acc[:, t, ns])
+
+        def to_tiles(c, q):
+            ps = ps_in.tile([P, TILES_GROUP, P], F32, tag="in")
+            for i in range(TILES_GROUP):
+                z = z_tiles[:, c, TILES_GROUP * q + i].rearrange("p e j -> p (e j)")
+                nc.tensor.transpose(ps[:, i, :], z, ident[:])
+            width = A_TENSOR if c == A else P
+            src = ps[:, :, 0:width].rearrange("p i (g c) -> p i g c", c=GROUP)
+            softmax((c, q), twork, "a" if c == A else "t", src, TILES_GROUP, width // GROUP)
+
+        def normalise_tiles(c, q):
+            tiles = slice(TILES_GROUP * q, TILES_GROUP * (q + 1))
+            dst = {A: y_ab[:, tiles, P:AB], BB: y_ab[:, tiles, 0:P], C: y_c[:, tiles, :]}[c]
+            engine = nc.vector if (c, q) == SOFTMAXES[-1] else nc.gpsimd
+            normalise(soft[c, q], engine, dst.rearrange("p i (g c) -> p i g c", c=GROUP))
+
+        def combine(y, tiles, col):
+            width = y.shape[2]
+            ps = ps_out.tile([P, len(tiles), width], F32, tag="out")
+            for i, t in enumerate(tiles):
+                nc.tensor.matmul(out=ps[:, i, :], lhsT=diag[:, t, :], rhs=y[:, t, :], start=True, stop=True)
+
+            def finish():
+                res = twork.tile([P, len(tiles), width], F32, tag="o%d" % width)
+                nc.scalar.copy(out=res[:], in_=ps[:])
+                rows = out2d[tiles[0] * P : (tiles[-1] + 1) * P, col : col + width]
+                nc.sync.dma_start(out=rows.rearrange("(t p) l -> p t l", p=P), in_=res[:])
+
+            return finish
+
+        def park_route():
             nc.sync.dma_start(
                 out=out.rearrange("(t p) n l -> p t n l", p=P)[:, :, 0, 0 : E * N],
-                in_=comb[:].rearrange("p t e n -> p t (e n)"),
+                in_=route[:].rearrange("p t e n -> p t (e n)"),
             )
 
-        def load_c(j):
-            rows = out.rearrange("(t j) n l -> j t n l", j=16)[j, :, 0, 0 : E * N]
-            nc.sync.dma_start(
-                out=c_sb[j : P : 16, :, j * N : (j + 1) * N],
-                in_=rows.rearrange("t (e n) -> e t n", e=E),
-            )
-
-        def t2(c, q):
-            zq = psA.tile([P, 4, P], F32, tag="A")
-            for i in range(4):
-                nc.tensor.transpose(zq[:, i, :], zT[:, c, 4 * q + i].rearrange("p e j -> p (e j)"), ident[:])
-            w = VO if c == CA else P
-            pt[c, q] = sm_new(
-                pwork, "p%d" % (c == CA), zq[:, :, 0:w].rearrange("p i (g c) -> p i g c", c=G8), 4, w // G8
-            )
-
-        def ml(c, q, eng):
-            t0 = slice(4 * q, 4 * q + 4)
-            dst = y_c[:, t0, :] if c == CC else y_ab[:, t0, 0:P] if c == CB else y_ab[:, t0, P:LAB]
-            f_mul(pt[c, q], eng, dst.rearrange("p i (g c) -> p i g c", c=G8))
-
-        def mm_ab(k):
-            op = psC.tile([P, 2, LAB], F32, tag="C")
-            for i in range(2):
-                t = 2 * k + i
-                nc.tensor.matmul(out=op[:, i, :], lhsT=c_sb[:, t, :], rhs=y_ab[:, t, :], start=True, stop=True)
-            return op
-
-        def cp_ab(k, op):
-            osb = pwork.tile([P, 2, LAB], F32, tag="oab")
-            nc.scalar.copy(out=osb[:], in_=op[:])
-            rows = out2d[2 * k * P : (2 * k + 2) * P, P : P + LAB]
-            nc.sync.dma_start(out=rows.rearrange("(t p) l -> p t l", p=P), in_=osb[:])
-
-        def mm_c(q):
-            op = psC.tile([P, 4, P], F32, tag="C")
-            for i in range(4):
-                t = 4 * q + i
-                nc.tensor.matmul(out=op[:, i, :], lhsT=c_sb[:, t, :], rhs=y_c[:, t, :], start=True, stop=True)
-            return op
-
-        def cp_c(q, op):
-            osb = pwork.tile([P, 4, P], F32, tag="oc")
-            nc.scalar.copy(out=osb[:], in_=op[:])
-            rows = out2d[4 * q * P : (4 * q + 4) * P, 0:P]
-            nc.sync.dma_start(out=rows.rearrange("(t p) l -> p t l", p=P), in_=osb[:])
-
-        load_h(0)
-        nc.sync.dma_start(out=lg_b[:], in_=logits.rearrange("(t p) n e -> p t n e", p=P))
-        load_w(0)
-        load_h(1)
-        nc.vector.memset(bz[:], 0.0)
-        nc.sync.dma_start(out=bz[0 : 3 * E, :], in_=b3.rearrange("e (t l) -> (e t) l", l=P))
-        load_w(1)
-        load_h(2)
-        load_w(2)
-        load_h(3)
-        load_w(3)
-        make_identity(nc, ident[:])
-        nc.gpsimd.memset(c_sb[:], 0.0)
-        warm = const.tile([P, 1], F32)
-        nc.vector.memset(warm[:], 0.0)
-        nc.scalar.activation(out=warm[:], in_=warm[:], func=ACT.Exp)
-        th(0)
-        load_h(4)
-        load_w(4)
-        sa = sm_new(vwork, "a", lg_b[:], BT, N)
-        f_max(sa)
-        f_sub(sa)
-        ch(0)
-        f_exp(sa)
-        th(1)
-        load_h(5)
-        load_w(5)
-        rg(SLOTS[0], False)
-        nc.vector.tensor_copy(out=bz32[:], in_=bz[:])
+        def load_diag():
+            for j in range(ROWS):
+                parked = out.rearrange("(t j) n l -> j t n l", j=ROWS)[j, :, 0, 0 : E * N]
+                nc.sync.dma_start(
+                    out=diag[j:P:ROWS, :, j * N : (j + 1) * N],
+                    in_=parked.rearrange("t (e n) -> e t n", e=E),
+                )
 
         due = {}
 
-        def at(i, what, *args):
-            due.setdefault((i, what), []).append(args)
+        def at(slot, what, *args):
+            due.setdefault((slot, what), []).append(args)
+
+        def softmax_at(slot, key, transposes, *args):
+            at(slot - 1, "transposes", transposes, *args)
+            at(slot, "start", key)
+            at(slot + EXP, "exponential", key)
+            at(slot + NORM, "end", key)
 
         for k in range(E // 2):
-            s = SLOTS.index((CA, 2 * k + 1)) + V_LAG
-            at(s - 1, "tv", k)
-            at(s, "new", "v", k)
-            at(s + X_LAG, "exp", "v", k)
-            at(s + S_LAG, "old", "v", k)
-        nexti = 0
-        groups = [(c, q) for q in range(4) for c in (CA, CB)] + [(CC, q) for q in range(4)]
-        for c, q in groups:
-            nexti = max(SLOTS.index((c, E - 1)) + V_LAG, nexti)
-            for s in (nexti,):
-                at(s - 1, "t2", c, q)
-                at(s, "new", "p", (c, q))
-                at(s + X_LAG, "exp", "p", (c, q))
-                at(s + S_LAG, "old", "p", (c, q))
-                if c == CB:
-                    for k in (2 * q, 2 * q + 1):
-                        at(s + S_LAG + M_LAG, "mm", mm_ab, cp_ab, k)
-                        at(s + S_LAG + M_LAG + 1, "cp", k)
-                if c == CC:
-                    at(s + S_LAG + M_LAG, "mm", mm_c, cp_c, q)
-                    at(s + S_LAG + M_LAG + 1, "cp", NT + q)
-                nexti += P_EVERY[c]
-        end = max(i for i, w in due) + 1
-        ops, stts = {}, []
-        chain = {"v": vt, "p": pt}
+            softmax_at(SLOTS.index((A, 2 * k + 1)) + START, ("rows", k), to_rows, k)
+        slot = SLOTS.index((BB, E - 1)) + START_AB
+        for c, q in SOFTMAXES:
+            if c == C:
+                slot = max(slot, SLOTS.index((C, E - 1)) + START)
+            softmax_at(slot, (c, q), to_tiles, c, q)
+            if c == BB:
+                for k in (2 * q, 2 * q + 1):
+                    at(slot + MATMUL, "combine", y_ab, [2 * k, 2 * k + 1], P)
+            if c == C:
+                at(slot + MATMUL, "combine", y_c, list(range(TILES_GROUP * q, TILES_GROUP * (q + 1))), 0)
+            slot += 1
+        last = max(i for i, what in due) + 1
 
-        def fill(count, queue):
-            for u in range(min(count, len(stts))):
-                e, t, n = stts.pop(0)
-                v_stt(e, t, n)
-                if e == E - 1 and n % N_ST == N_ST - 1:
-                    ns = slice(n + 1 - N_ST, n + 1)
-                    queue.dma_start(out=out[t * P : (t + 1) * P, ns, LS:L], in_=acc[:, t, ns])
+        load_h(0)
+        nc.sync.dma_start(out=lg[:], in_=logits.rearrange("(t p) n e -> p t n e", p=P))
+        load_w(0)
+        nc.vector.memset(b_rows[:], 0.0)
+        nc.sync.dma_start(out=b_rows[0 : 3 * E, :], in_=b3.rearrange("e (t l) -> (e t) l", l=P))
+        load_h(1)
+        load_w(1)
+        for e in (2, 3):
+            load_h(e)
+            load_w(e)
+        make_identity(nc, ident[:])
+        nc.gpsimd.memset(diag[:], 0.0)
+        warm = const.tile([P, 1], F32)
+        nc.vector.memset(warm[:], 0.0)
+        nc.scalar.activation(out=warm[:], in_=warm[:], func=ACT.Exp)
+        transpose_h(0)
+        load_h(4)
+        load_w(4)
+        softmax("route", vwork, "r", lg[:], HALVES, N)
+        routing = soft["route"]
+        reduce_to(routing, "max", lg[:], ALU.max)
+        subtract(routing)
+        copy_h(0)
+        exponential(routing)
+        transpose_h(1)
+        load_h(5)
+        load_w(5)
+        regroup_w(SLOTS[0], False)
+        nc.vector.tensor_copy(out=b_rows32[:], in_=b_rows[:])
 
-        for i in range(max(end, len(SLOTS) + 1)):
-            nxt = SLOTS[i + 1] if i + 1 < len(SLOTS) else None
-            cur = SLOTS[i] if i < len(SLOTS) else None
-            prv = SLOTS[i - 1] if 0 <= i - 1 < len(SLOTS) else None
-            if prv:
-                mx(prv)
+        finishes = []
+        for i in range(last + 1):
+            before, unit, after, later = [SLOTS[s] if 0 <= s < len(SLOTS) else None for s in range(i - 1, i + 3)]
+            if before:
+                multiply(before)
             if i == 0:
-                pb = psC.tile([P, P], F32, tag="C")
-                nc.tensor.transpose(pb[:], bz32[:], ident[:])
-            for w in S_ORDER:
-                if w == "c" and nxt and nxt[0] == CA and nxt[1] > 0:
-                    ch(nxt[1])
-                if w == "r" and nxt:
-                    rg(nxt, False)
-                if w == "e" and prv:
-                    e1(prv)
-                if w == "x":
-                    for kind, k in due.get((i, "exp"), []):
-                        f_exp(chain[kind][k])
-                if w == "p":
-                    for (k,) in due.get((i, "cp"), []):
-                        cpf, kk, op = ops.pop(k)
-                        cpf(kk, op)
-            if i + 2 < len(SLOTS) and SLOTS[i + 2][0] == CA and SLOTS[i + 2][1] > 1:
-                e = SLOTS[i + 2][1]
-                th(e)
+                b_ps = ps_out.tile([P, P], F32, tag="out")
+                nc.tensor.transpose(b_ps[:], b_rows32[:], ident[:])
+            if after and after[0] == A:
+                copy_h(after[1])
+            for (key,) in due.get((i, "exponential"), []):
+                exponential(soft[key])
+            if after:
+                regroup_w(after, False)
+            if before:
+                add_bias(before)
+            for finish in finishes:
+                finish()
+            if later and later[0] == A and later[1] > 1:
+                e = later[1]
+                transpose_h(e)
                 if e + 4 < E:
                     load_h(e + 4)
                     load_w(e + 4)
-            for (k,) in due.get((i, "tv"), []):
-                tv_(k)
-            for c, q in due.get((i, "t2"), []):
-                t2(c, q)
-            for f, cpf, k in due.get((i, "mm"), []):
-                ops[k + (NT if cpf is cp_c else 0)] = (cpf, k, f(k))
-            if i == C_FROM:
-                for j in range(16):
-                    load_c(j)
-            new = [chain[kind][k] for kind, k in due.get((i, "new"), [])]
-            old = [chain[kind][k] for kind, k in due.get((i, "old"), [])]
-            if cur:
+            for transposes, *args in due.get((i, "transposes"), []):
+                transposes(*args)
+            finishes = [combine(*args) for args in due.get((i, "combine"), [])]
+            if unit == (BB, E - 1):
+                load_diag()
+            starts = [soft[key] for (key,) in due.get((i, "start"), [])]
+            ends = [soft[key] for (key,) in due.get((i, "end"), [])]
+            if unit:
                 if i == 0:
-                    rg(cur, True)
-                if cur[0] == CA:
-                    qh(cur[1])
-                qw(cur)
-            for o in old:
-                f_sum(o)
-            for o in new:
-                f_max(o)
-            if nxt:
-                rg(nxt, True)
-            for o in old:
-                f_rec(o)
-            for o in new:
-                f_sub(o)
+                    regroup_w(unit, True)
+                if unit[0] == A:
+                    quantise_h(unit[1])
+                quantise_w(unit)
+            for o in ends:
+                reduce_to(o, "sum", o["e"][:], ALU.add)
+            for o in starts:
+                reduce_to(o, "max", o["src"], ALU.max)
+            if after:
+                regroup_w(after, True)
+            for o in ends:
+                reciprocal(o)
+            for o in starts:
+                subtract(o)
             if i == 0:
-                f_sum(sa)
-                f_rec(sa)
+                reduce_to(routing, "sum", routing["e"][:], ALU.add)
+                reciprocal(routing)
                 nc.vector.tensor_tensor(
-                    out=comb[:],
-                    in0=sa["e"][:].rearrange("p t n e -> p t e n"),
-                    in1=sa["r"][:].unsqueeze(2).to_broadcast([P, BT, E, N]),
+                    out=route[:],
+                    in0=routing["e"][:].rearrange("p t n e -> p t e n"),
+                    in1=routing["r"][:].unsqueeze(2).to_broadcast([P, HALVES, E, N]),
                     op=ALU.mult,
                 )
-                park()
-                nc.vector.tensor_copy(out=b3T[:], in_=pb[:, 0 : 3 * E])
-            for kind, k in due.get((i, "old"), []):
-                if kind == "v":
-                    f_mul(vt[k], nc.vector, vt[k]["e"][:])
-                    stts.extend([(2 * k + d, t, n) for d in range(2) for t in range(BT) for n in range(N)])
-                    if k == E // 2 - 1:
-                        stts[:] = sorted(stts, key=lambda s: (s[1], s[2] // N_ST, s[0], s[2]))
-                else:
-                    ml(*k, nc.vector if k in V_MUL else nc.gpsimd)
-            fill(max(0, min(F3, len(stts) - KEEP)), nc.sync)
-        fill(1000, nc.scalar)
+                park_route()
+                nc.vector.tensor_copy(out=bias[:], in_=b_ps[:, 0 : 3 * E])
+            for (key,) in due.get((i, "end"), []):
+                if key[0] != "rows":
+                    normalise_tiles(*key)
+                    continue
+                normalise(soft[key], nc.vector, soft[key]["e"][:])
+                k = key[1]
+                adds.extend((2 * k + d, t, n) for d in range(2) for t in range(HALVES) for n in range(N))
+                if k == E // 2 - 1:
+                    adds[:] = sorted(adds, key=lambda s: (s[1], s[2] // AGENTS_A_STORE, s[0], s[2]))
+            multiply_adds(max(0, min(ADDS_A_SLOT, len(adds) - ADDS_KEPT)), nc.sync)
+        multiply_adds(len(adds), nc.scalar)

@@ -37,7 +37,7 @@ START_AB = 4
 SOFTMAXES = [(c, q) for h in range(2) for c in (A, BB) for q in (2 * h, 2 * h + 1)] + [(C, q) for q in range(TILES // TILES_GROUP)]
 ADDS_A_SLOT = N
 ADDS_KEPT = 5 * N
-AGENTS_A_STORE = 2
+AGENTS_A_STORE = 4
 
 
 def wide(ap, a, g):
@@ -350,6 +350,8 @@ def tile_softmoedynamics_pb_kernel(tc, h2, logits, W3, b3, out):
             finishes = [combine(*args) for args in due.get((i, "combine"), [])]
             if unit == (BB, E - 1):
                 load_diag()
+            if i == len(SLOTS):
+                ctx.enter_context(tc.manual_schedule(engines={ENG.DVE}))
             starts = [soft[key] for (key,) in due.get((i, "start"), [])]
             ends = [soft[key] for (key,) in due.get((i, "end"), [])]
             if unit:

from contextlib import ExitStack

import concourse.mybir as mybir
from concourse.masks import make_identity

F32 = mybir.dt.float32
BF16 = mybir.dt.bfloat16
U32 = mybir.dt.uint32
U8 = mybir.dt.uint8
FP8X4 = mybir.dt.float8_e4m3fn_x4
ALU = mybir.AluOpType
ACT = mybir.ActivationFunctionType
AX = mybir.AxisListType
ENG = mybir.EngineType

P = 128
B, N, E, L, H2 = 256, 8, 8, 384, 1024
GROUP = 8
HALVES = B // P
PASSES = 2
QUAD = 4
ROWS = P // E
TILES = B // ROWS
TILES_GROUP = 4

A, BB, C = 2, 1, 0
A_TENSOR = 48
LV = P - A_TENSOR
AB = P + A_TENSOR

SLOTS = [(c, e) for e in range(E) for c in (A, BB)] + [(C, e) for e in range(E)]
ON_VECTOR = [(A, 0)] + [(BB, e) for e in range(1, E - 1)]

EXP, NORM, MATMUL = 1, 2, 4
START = 3
START_AB = 4
SOFTMAXES = [(c, q) for h in range(2) for c in (A, BB) for q in (2 * h, 2 * h + 1)] + [(C, q) for q in range(TILES // TILES_GROUP)]
ADDS_A_SLOT = N
ADDS_KEPT = 5 * N
AGENTS_A_STORE = 4


def wide(ap, a, g):
    return ap.unsqueeze(3).to_broadcast([P, a, g, GROUP])


def tile_softmoedynamics_pb_kernel(tc, h2, logits, W3, b3, out):
    nc = tc.nc
    with ExitStack() as ctx:
        ctx.enter_context(tc.manual_schedule(engines={ENG.PE, ENG.Activation, ENG.SP, ENG.Pool}))
        const = ctx.enter_context(tc.tile_pool(name="const", bufs=1))
        raw_h = ctx.enter_context(tc.tile_pool(name="raw_h", bufs=4))
        raw_w = ctx.enter_context(tc.tile_pool(name="raw_w", bufs=E))
        stage = ctx.enter_context(tc.tile_pool(name="stage", bufs=3))
        codes = ctx.enter_context(tc.tile_pool(name="codes", bufs=E))
        vwork = ctx.enter_context(tc.tile_pool(name="vwork", bufs=3))
        twork = ctx.enter_context(tc.tile_pool(name="twork", bufs=4))
        ps_in = ctx.enter_context(tc.psum_pool(name="ps_in", bufs=3))
        ps_z = ctx.enter_context(tc.psum_pool(name="ps_z", bufs=2))
        ps_out = ctx.enter_context(tc.psum_pool(name="ps_out", bufs=3))

        ident = const.tile([P, P], F32)
        b_rows = const.tile([P, P], BF16)
        b_rows32 = const.tile([P, P], F32)
        bias = const.tile([P, 3 * E], F32)
        lg = const.tile([P, HALVES, N, E], BF16)
        route = const.tile([P, HALVES, E, N], F32)
        diag = const.tile([P, TILES, P], F32)
        z_tiles = const.tile([P, 3, TILES, E, ROWS], F32)
        z_rows = const.tile([P, E, B], F32)
        y_ab = const.tile([P, TILES, AB], F32)
        y_c = const.tile([P, TILES, P], F32)
        acc = const.tile([P, HALVES, N, LV], F32)
        h_raw, h_ps, h_grp, h_mx = {}, {}, {}, {}
        w_raw, w_grp, w_mx, z_ps = {}, {}, {}, {}
        soft = {}
        out2d = out.rearrange("b n l -> (b n) l")

        def load_h(e):
            raw = raw_h.tile([P, HALVES * H2], BF16, tag="h")
            h_raw[e] = raw
            nc.sync.dma_start(
                out=raw[:].rearrange("p (t k) -> p t k", t=HALVES),
                in_=h2[:, e, :].rearrange("(t p) k -> p t k", p=P),
            )

        def load_w(e):
            raw = raw_w.tile([P, PASSES, QUAD, L], BF16, tag="w")
            w_raw[e] = raw
            nc.sync.dma_start(
                out=raw[:].rearrange("p g c w -> p g (c w)"),
                in_=W3[e].rearrange("(g p c) w -> p g (c w)", g=PASSES, p=P, c=QUAD),
            )

        def transpose_h(e):
            words = h_raw[e][:].bitcast(F32)
            half, one_pass = H2 // 2, H2 // 2 // PASSES
            h_ps[e] = []
            for g in range(PASSES):
                ps = ps_in.tile([P, 2, B], F32, tag="in")
                for u in range(2):
                    for t in range(HALVES):
                        c0 = t * half + g * one_pass
                        nc.tensor.transpose(
                            ps[:, u, t * P : (t + 1) * P], words[:, c0 + u : c0 + one_pass : 2], ident[:]
                        )
                h_ps[e].append(ps)

        def copy_h(e):
            grp = stage.tile([P, QUAD * PASSES * B], BF16, tag="h", align_bytes=64)
            h_grp[e] = grp
            dst = grp[:].bitcast(F32).rearrange("p (g b u) -> p g b u", g=PASSES, u=2)
            for g in range(PASSES):
                nc.scalar.copy(out=dst[:, g], in_=h_ps[e][g][:].rearrange("p u b -> p b u"))

        def quantise_h(e):
            c = codes.tile([P, PASSES * B], U32, tag="hc", align_bytes=64)
            s = codes.tile([P, PASSES * B], U8, tag="hs", align_bytes=64)
            nc.vector.quantize_mx(out=c[:].bitcast(FP8X4), scales=s[:], in_=h_grp[e][:])
            h_mx[e] = (c, s)

        def regroup_w(unit, vector):
            if (unit in ON_VECTOR) != vector:
                return
            c, e = unit
            grp = stage.tile([P, PASSES, QUAD * P], BF16, tag="w", align_bytes=64)
            w_grp[unit] = grp
            for g in range(PASSES):
                dst = grp[:, g].rearrange("p (c i t) -> p c t i", i=4, t=QUAD)
                src = w_raw[e][:, g, :, c * P : (c + 1) * P].rearrange("p t (c i) -> p c t i", i=4)
                if vector:
                    nc.vector.tensor_copy(out=dst, in_=src)
                else:
                    nc.scalar.copy(out=dst, in_=src)

        def quantise_w(unit):
            c = stage.tile([P, PASSES * P], U32, tag="wc", align_bytes=64)
            s = stage.tile([P, PASSES * P], U8, tag="ws", align_bytes=64)
            nc.vector.quantize_mx(
                out=c[:].bitcast(FP8X4), scales=s[:], in_=w_grp[unit][:].rearrange("p g n -> p (g n)")
            )
            w_mx[unit] = (c, s)

        def multiply(unit):
            (hc, hs), (wc, ws) = h_mx[unit[1]], w_mx[unit]
            z = ps_z.tile([P, B], F32, tag="z")
            z_ps[unit] = z
            for g in range(PASSES):
                w_cols, h_cols = slice(g * P, (g + 1) * P), slice(g * B, (g + 1) * B)
                nc.tensor.matmul_mx(
                    out=z[:],
                    lhsT=wc[:, w_cols].bitcast(FP8X4),
                    lhsT_scale=ws[:, w_cols],
                    rhs=hc[:, h_cols].bitcast(FP8X4),
                    rhs_scale=hs[:, h_cols],
                    start=(g == 0),
                    stop=(g == PASSES - 1),
                )

        def add_bias(unit):
            c, e = unit
            z, b = z_ps[unit], bias[:, 3 * e + c : 3 * e + c + 1]
            if c == A:
                nc.scalar.activation(out=z_rows[:, e, :], in_=z[:], func=ACT.Identity, bias=b, scale=1.0)
            nc.scalar.activation(
                out=z_tiles[:, c, :, e, :],
                in_=z[:].rearrange("p (t j) -> p t j", j=ROWS),
                func=ACT.Identity,
                bias=b,
                scale=1.0,
            )

        def softmax(key, pool, tag, src, a, g):
            soft[key] = {"pool": pool, "tag": tag, "src": src, "shape": [P, a, g]}

        def reduce_to(o, name, src, op):
            res = o["pool"].tile(o["shape"], F32, tag=o["tag"] + name)
            nc.vector.tensor_reduce(out=res[:], in_=src, axis=AX.X, op=op)
            o[name] = res

        def subtract(o):
            _, a, g = o["shape"]
            res = o["pool"].tile([P, a, g, GROUP], F32, tag=o["tag"] + "e")
            o["e"] = res
            nc.vector.tensor_tensor(out=res[:], in0=o["src"], in1=wide(o["max"][:], a, g), op=ALU.subtract)

        def exponential(o):
            nc.scalar.activation(out=o["e"][:], in_=o["e"][:], func=ACT.Exp)

        def reciprocal(o):
            res = o["pool"].tile(o["shape"], F32, tag=o["tag"] + "r")
            nc.vector.reciprocal(out=res[:], in_=o["sum"][:])
            o["r"] = res

        def normalise(o, engine, dst):
            _, a, g = o["shape"]
            engine.tensor_tensor(out=dst, in0=o["e"][:], in1=wide(o["r"][:], a, g), op=ALU.mult)

        def to_rows(k):
            ps = ps_out.tile([P, 2, HALVES, P], F32, tag="out")
            for d in range(2):
                for t in range(HALVES):
                    nc.tensor.transpose(ps[:, d, t, :], z_rows[:, 2 * k + d, t * P : (t + 1) * P], ident[:])
            src = ps[:, :, :, A_TENSOR:P].rearrange("p d t (g c) -> p (d t) g c", c=GROUP)
            softmax(("rows", k), vwork, "v", src, 2 * HALVES, LV // GROUP)

        def multiply_add(e, t, n):
            y = soft["rows", e // 2]["e"][:, (e % 2) * HALVES + t].rearrange("p g c -> p (g c)")
            weight, a = route[:, t, e, n : n + 1], acc[:, t, n, :]
            if e == 0:
                nc.vector.tensor_scalar_mul(out=a, in0=y, scalar1=weight)
            else:
                nc.vector.scalar_tensor_tensor(out=a, in0=y, scalar=weight, in1=a, op0=ALU.mult, op1=ALU.add)

        adds = []

        def multiply_adds(count, queue):
            for _ in range(count):
                e, t, n = adds.pop(0)
                multiply_add(e, t, n)
                if e == E - 1 and n % AGENTS_A_STORE == AGENTS_A_STORE - 1:
                    ns = slice(n + 1 - AGENTS_A_STORE, n + 1)
                    queue.dma_start(out=out[t * P : (t + 1) * P, ns, L - LV : L], in_=acc[:, t, ns])

        def to_tiles(c, q):
            ps = ps_in.tile([P, TILES_GROUP, P], F32, tag="in")
            for i in range(TILES_GROUP):
                z = z_tiles[:, c, TILES_GROUP * q + i].rearrange("p e j -> p (e j)")
                nc.tensor.transpose(ps[:, i, :], z, ident[:])
            width = A_TENSOR if c == A else P
            src = ps[:, :, 0:width].rearrange("p i (g c) -> p i g c", c=GROUP)
            softmax((c, q), twork, "a" if c == A else "t", src, TILES_GROUP, width // GROUP)

        def normalise_tiles(c, q):
            tiles = slice(TILES_GROUP * q, TILES_GROUP * (q + 1))
            dst = {A: y_ab[:, tiles, P:AB], BB: y_ab[:, tiles, 0:P], C: y_c[:, tiles, :]}[c]
            engine = nc.vector if (c, q) == SOFTMAXES[-1] else nc.gpsimd
            normalise(soft[c, q], engine, dst.rearrange("p i (g c) -> p i g c", c=GROUP))

        def combine(y, tiles, col):
            width = y.shape[2]
            ps = ps_out.tile([P, len(tiles), width], F32, tag="out")
            for i, t in enumerate(tiles):
                nc.tensor.matmul(out=ps[:, i, :], lhsT=diag[:, t, :], rhs=y[:, t, :], start=True, stop=True)

            def finish():
                res = twork.tile([P, len(tiles), width], F32, tag="o%d" % width)
                nc.scalar.copy(out=res[:], in_=ps[:])
                rows = out2d[tiles[0] * P : (tiles[-1] + 1) * P, col : col + width]
                nc.sync.dma_start(out=rows.rearrange("(t p) l -> p t l", p=P), in_=res[:])

            return finish

        def park_route():
            nc.sync.dma_start(
                out=out.rearrange("(t p) n l -> p t n l", p=P)[:, :, 0, 0 : E * N],
                in_=route[:].rearrange("p t e n -> p t (e n)"),
            )

        def load_diag():
            for j in range(ROWS):
                parked = out.rearrange("(t j) n l -> j t n l", j=ROWS)[j, :, 0, 0 : E * N]
                nc.sync.dma_start(
                    out=diag[j:P:ROWS, :, j * N : (j + 1) * N],
                    in_=parked.rearrange("t (e n) -> e t n", e=E),
                )

        due = {}

        def at(slot, what, *args):
            due.setdefault((slot, what), []).append(args)

        def softmax_at(slot, key, transposes, *args):
            at(slot - 1, "transposes", transposes, *args)
            at(slot, "start", key)
            at(slot + EXP, "exponential", key)
            at(slot + NORM, "end", key)

        for k in range(E // 2):
            softmax_at(SLOTS.index((A, 2 * k + 1)) + START, ("rows", k), to_rows, k)
        slot = SLOTS.index((BB, E - 1)) + START_AB
        for c, q in SOFTMAXES:
            if c == C:
                slot = max(slot, SLOTS.index((C, E - 1)) + START)
            softmax_at(slot, (c, q), to_tiles, c, q)
            if c == BB:
                for k in (2 * q, 2 * q + 1):
                    at(slot + MATMUL, "combine", y_ab, [2 * k, 2 * k + 1], P)
            if c == C:
                at(slot + MATMUL, "combine", y_c, list(range(TILES_GROUP * q, TILES_GROUP * (q + 1))), 0)
            slot += 1
        last = max(i for i, what in due) + 1

        load_h(0)
        nc.sync.dma_start(out=lg[:], in_=logits.rearrange("(t p) n e -> p t n e", p=P))
        load_w(0)
        nc.vector.memset(b_rows[:], 0.0)
        nc.sync.dma_start(out=b_rows[0 : 3 * E, :], in_=b3.rearrange("e (t l) -> (e t) l", l=P))
        load_h(1)
        load_w(1)
        for e in (2, 3):
            load_h(e)
            load_w(e)
        make_identity(nc, ident[:])
        nc.gpsimd.memset(diag[:], 0.0)
        warm = const.tile([P, 1], F32)
        nc.vector.memset(warm[:], 0.0)
        nc.scalar.activation(out=warm[:], in_=warm[:], func=ACT.Exp)
        transpose_h(0)
        load_h(4)
        load_w(4)
        softmax("route", vwork, "r", lg[:], HALVES, N)
        routing = soft["route"]
        reduce_to(routing, "max", lg[:], ALU.max)
        subtract(routing)
        copy_h(0)
        exponential(routing)
        transpose_h(1)
        load_h(5)
        load_w(5)
        regroup_w(SLOTS[0], False)
        nc.vector.tensor_copy(out=b_rows32[:], in_=b_rows[:])

        finishes = []
        for i in range(last + 1):
            before, unit, after, later = [SLOTS[s] if 0 <= s < len(SLOTS) else None for s in range(i - 1, i + 3)]
            if before:
                multiply(before)
            if i == 0:
                b_ps = ps_out.tile([P, P], F32, tag="out")
                nc.tensor.transpose(b_ps[:], b_rows32[:], ident[:])
            if after and after[0] == A:
                copy_h(after[1])
            for (key,) in due.get((i, "exponential"), []):
                exponential(soft[key])
            if after:
                regroup_w(after, False)
            if before:
                add_bias(before)
            for finish in finishes:
                finish()
            if later and later[0] == A and later[1] > 1:
                e = later[1]
                transpose_h(e)
                if e + 4 < E:
                    load_h(e + 4)
                    load_w(e + 4)
            for transposes, *args in due.get((i, "transposes"), []):
                transposes(*args)
            finishes = [combine(*args) for args in due.get((i, "combine"), [])]
            if unit == (BB, E - 1):
                load_diag()
            if i == len(SLOTS):
                ctx.enter_context(tc.manual_schedule(engines={ENG.DVE}))
            starts = [soft[key] for (key,) in due.get((i, "start"), [])]
            ends = [soft[key] for (key,) in due.get((i, "end"), [])]
            if unit:
                if i == 0:
                    regroup_w(unit, True)
                if unit[0] == A:
                    quantise_h(unit[1])
                quantise_w(unit)
            for o in ends:
                reduce_to(o, "sum", o["e"][:], ALU.add)
            for o in starts:
                reduce_to(o, "max", o["src"], ALU.max)
            if after:
                regroup_w(after, True)
            for o in ends:
                reciprocal(o)
            for o in starts:
                subtract(o)
            if i == 0:
                reduce_to(routing, "sum", routing["e"][:], ALU.add)
                reciprocal(routing)
                nc.vector.tensor_tensor(
                    out=route[:],
                    in0=routing["e"][:].rearrange("p t n e -> p t e n"),
                    in1=routing["r"][:].unsqueeze(2).to_broadcast([P, HALVES, E, N]),
                    op=ALU.mult,
                )
                park_route()
                nc.vector.tensor_copy(out=bias[:], in_=b_ps[:, 0 : 3 * E])
            for (key,) in due.get((i, "end"), []):
                if key[0] != "rows":
                    normalise_tiles(*key)
                    continue
                normalise(soft[key], nc.vector, soft[key]["e"][:])
                k = key[1]
                adds.extend((2 * k + d, t, n) for d in range(2) for t in range(HALVES) for n in range(N))
                if k == E // 2 - 1:
                    adds[:] = sorted(adds, key=lambda s: (s[1], s[2] // AGENTS_A_STORE, s[0], s[2]))
            multiply_adds(max(0, min(ADDS_A_SLOT, len(adds) - ADDS_KEPT)), nc.sync)
        multiply_adds(len(adds), nc.scalar)
